import numpy as np
import ml_dtypes


def mxq(x, axis, fmt="e4m3"):
    dtype, down = {"e4m3": (ml_dtypes.float8_e4m3fn, 7), "e5m2": (ml_dtypes.float8_e5m2, 14)}[fmt]
    v = np.moveaxis(np.asarray(x, np.float32).astype(ml_dtypes.bfloat16).astype(np.float64), axis, -1)
    blocks = v.reshape(v.shape[:-1] + (-1, 32))
    amax = np.abs(blocks).max(-1, keepdims=True)
    byte = np.maximum(np.where(amax > 0, np.frexp(amax)[1] - 1 + 127, 0) - down, 1)
    scale = np.exp2(byte - 127.0)
    codes = (blocks / scale).astype(np.float32).astype(dtype).astype(np.float64)
    return np.moveaxis((codes * scale).reshape(v.shape), -1, axis)


WIDE = False


def mx_kscale(k):
    if not WIDE:
        return np.ones(k)
    levels = np.array([10, -10, 5, -5, 0])
    a = np.random.permutation(np.resize(levels, k // 512 * 4)).reshape(k // 512, 4)
    idx = np.arange(k)
    return np.exp2(a[idx // 512, idx % 128 // 32])


BF16 = ml_dtypes.bfloat16


def bf(x):
    return np.asarray(x, np.float32).astype(BF16)


def f64(x):
    return np.asarray(x).astype(np.float64)


N, TQ, TS, C, E = 4, 2048, 512, 512, 512
SQRT_HALF = np.sqrt(0.5)


def wn_weight(v, g):
    return g[:, None] * v / np.sqrt((v * v).sum(axis=1, keepdims=True))


def setup_inputs():
    t = mx_kscale(E)
    return {
        "x": bf(np.random.standard_normal((N, TQ, C))),
        "target_embedding": bf(np.random.standard_normal((N, TQ, E)) * t),
        "encoder_keys": bf(np.random.standard_normal((N, E, TS)) * 1.5 / np.sqrt(E) / t[:, None]),
        "in_proj_v": bf(np.random.standard_normal((E, C)) * (0.5 + np.random.random((E, 1))) / np.sqrt(C)),
        "in_proj_g": bf((1.0 + 0.1 * np.random.standard_normal(E)) * t),
        "in_proj_b": bf(0.2 * np.random.standard_normal(E) * t),
    }


def reference(x, target_embedding, encoder_keys, in_proj_v, in_proj_g, in_proj_b):
    wi = wn_weight(f64(in_proj_v), f64(in_proj_g))
    h = ((mxq(f64(x), 2, "e4m3") @ mxq(wi, 1, "e4m3").T) + f64(in_proj_b) + f64(target_embedding)) * SQRT_HALF
    return mxq(h, 2, "e4m3") @ mxq(f64(encoder_keys), 1, "e4m3")

@@ -1,0 +1,341 @@
+from contextlib import ExitStack
+import math
+
+import concourse.mybir as mybir
+from concourse.masks import make_identity
+
+F32 = mybir.dt.float32
+BF16 = mybir.dt.bfloat16
+U32 = mybir.dt.uint32
+U8 = mybir.dt.uint8
+FP8X4 = mybir.dt.float8_e4m3fn_x4
+ACT = mybir.ActivationFunctionType
+ALU = mybir.AluOpType
+
+P = 128
+PACK = 4
+BATCH, TQ, TS, C, E = 4, 2048, 512, 512, 512
+BLOCKS = 4
+CHUNK = BLOCKS * P
+CHUNKS = BATCH * TQ // CHUNK
+CHUNKS_PER_ITEM = TQ // CHUNK
+SQRT_HALF = math.sqrt(0.5)
+
+X_AHEAD = 3
+TE_AHEAD = 2
+H_AHEAD = 1
+LOAD_AHEAD = 8
+X_BUFS = LOAD_AHEAD - X_AHEAD
+TE_BUFS = LOAD_AHEAD - TE_AHEAD
+
+FLOPS = 2 * BATCH * TQ * C * E + 2 * BATCH * TQ * E * TS
+
+
+def tile_attentionlayer_pa_t_kernel(
+    tc, x, target_embedding, encoder_keys, in_proj_v, in_proj_g, in_proj_b, out
+):
+    nc = tc.nc
+    x_rows = x.flatten_outer_dims()
+    te_rows = target_embedding.flatten_outer_dims()
+    out_rows = out.flatten_outer_dims()
+
+    with ExitStack() as ctx:
+        ctx.enter_context(tc.manual_schedule())
+
+        keep = ctx.enter_context(tc.tile_pool(name="keep", bufs=1))
+        x_pool = ctx.enter_context(tc.tile_pool(name="x_pool", bufs=X_BUFS))
+        te_pool = ctx.enter_context(tc.tile_pool(name="te_pool", bufs=TE_BUFS))
+        key_pool = ctx.enter_context(tc.tile_pool(name="key_pool", bufs=2))
+        two = ctx.enter_context(tc.tile_pool(name="two", bufs=2))
+        three = ctx.enter_context(tc.tile_pool(name="three", bufs=3))
+        psum = ctx.enter_context(tc.psum_pool(name="psum", bufs=2))
+
+        x_in, te_in, key_in = {}, {}, {}
+        x_grouped, x_codes, x_scales = {}, {}, {}
+        te_scaled = {}
+        h_grouped, h_codes, h_scales = {}, {}, {}
+        out_sb = {}
+
+        def live(c):
+            return 0 <= c < CHUNKS
+
+        def load_chunk(c):
+            rows = slice(c * CHUNK, (c + 1) * CHUNK)
+            x_in[c] = x_pool.tile([P, BLOCKS * C], BF16, name="x_in", tag="x_in")
+            nc.sync.dma_start(
+                out=x_in[c][:], in_=x_rows[rows, :].rearrange("(p j) c -> p (j c)", j=BLOCKS)
+            )
+            te_in[c] = te_pool.tile([P, BLOCKS * E], BF16, name="te_in", tag="te_in")
+            nc.sync.dma_start(
+                out=te_in[c][:], in_=te_rows[rows, :].rearrange("(p j) e -> p (j e)", j=BLOCKS)
+            )
+
+        def load_keys(n):
+            key_in[n] = key_pool.tile([P, PACK * TS], BF16, name="key_in", tag="key_in")
+            nc.sync.dma_start(
+                out=key_in[n][:].rearrange("q (half f) -> q half f", half=2),
+                in_=encoder_keys[n].rearrange("(half q par) s -> q half (par s)", half=2, par=2),
+            )
+
+        def store_chunk(c):
+            rows = slice(c * CHUNK, (c + 1) * CHUNK)
+            nc.sync.dma_start(
+                out=out_rows[rows, :].rearrange("(p j) s -> p (j s)", j=BLOCKS), in_=out_sb[c][:]
+            )
+
+        key_codes = keep.tile([P, BATCH * TS], U32, align_bytes=64)
+        key_scales = keep.tile([P, BATCH * TS], U8, align_bytes=64)
+        key_grouped = {}
+
+        def regroup_keys(n):
+            key_grouped[n] = key_pool.tile(
+                [P, TS * PACK], BF16, name="key_grouped", tag="key_grouped", align_bytes=64
+            )
+            nc.vector.tensor_copy(
+                out=key_grouped[n][:].rearrange("q (c i k) -> q c k i", i=4, k=PACK),
+                in_=key_in[n][:].rearrange("q (k c i) -> q c k i", k=PACK, i=4),
+            )
+
+        def quantise_keys(n):
+            cols = slice(n * TS, (n + 1) * TS)
+            nc.vector.quantize_mx(
+                out=key_codes[:, cols].bitcast(FP8X4),
+                scales=key_scales[:, cols],
+                in_=key_grouped[n][:],
+            )
+
+        def transpose_x(c, pair):
+            x_words = x_in[c][:].bitcast(F32)
+            bank = psum.tile([P, 4 * P], F32, name="xT", tag="xT")
+            for b in range(2):
+                for half in range(2):
+                    word0 = (2 * pair + b) * (C // 2) + half * P
+                    nc.tensor.transpose(
+                        bank[:, (2 * half + b) * P : (2 * half + b + 1) * P],
+                        x_words[:, word0 : word0 + P],
+                        ident_f32[:],
+                    )
+            return bank
+
+        def regroup_x(c, pair, bank):
+            if pair == 0:
+                x_grouped[c] = two.tile(
+                    [P, CHUNK * PACK], BF16, name="x_grouped", tag="x_grouped", align_bytes=64
+                )
+            words = x_grouped[c][:].bitcast(F32)
+            nc.vector.tensor_copy(
+                out=words[:, pair * 4 * P : (pair + 1) * 4 * P].rearrange(
+                    "q (r half) -> q r half", half=2
+                ),
+                in_=bank[:].rearrange("q (half r) -> q r half", half=2),
+            )
+
+        def quantise_x(c):
+            x_codes[c] = three.tile([P, CHUNK], U32, name="x_codes", tag="x_codes", align_bytes=64)
+            x_scales[c] = three.tile([P, CHUNK], U8, name="x_scales", tag="x_scales", align_bytes=64)
+            nc.vector.quantize_mx(
+                out=x_codes[c][:].bitcast(FP8X4), scales=x_scales[c][:], in_=x_grouped[c][:]
+            )
+
+        def transpose_te(c, half):
+            te_words = te_in[c][:].bitcast(F32)
+            bank = psum.tile([P, CHUNK], F32, name="teT", tag="teT")
+            for j in range(BLOCKS):
+                word0 = j * (E // 2) + half * P
+                nc.tensor.transpose(
+                    bank[:, j * P : (j + 1) * P], te_words[:, word0 : word0 + P], ident_f32[:]
+                )
+            return bank
+
+        def scale_te(c, half, bank):
+            if half == 0:
+                te_scaled[c] = two.tile([P, PACK, CHUNK], F32, name="te_scaled", tag="te_scaled")
+            pairs = bank[:].bitcast(BF16).rearrange("q (r par) -> q r par", par=2)
+            for par in range(2):
+                k = 2 * half + par
+                nc.scalar.activation(
+                    out=te_scaled[c][:, k, :],
+                    in_=pairs[:, :, par],
+                    func=ACT.Identity,
+                    bias=bias_scaled[:, k : k + 1],
+                    scale=SQRT_HALF,
+                )
+
+        def first_product(c, j):
+            block = slice(j * P, (j + 1) * P)
+            bank = psum.tile([P, PACK * P], F32, name="hT", tag="hT")
+            for k in range(PACK):
+                group = slice(k * P, (k + 1) * P)
+                nc.tensor.matmul_mx(
+                    out=bank[:, group],
+                    lhsT=w_codes[:, group].bitcast(FP8X4),
+                    lhsT_scale=w_scales[:, group],
+                    rhs=x_codes[c][:, block].bitcast(FP8X4),
+                    rhs_scale=x_scales[c][:, block],
+                    start=True,
+                    stop=True,
+                )
+            return bank
+
+        def form_h(c, j, bank):
+            if j == 0:
+                h_grouped[c] = two.tile(
+                    [P, CHUNK * PACK], BF16, name="h_grouped", tag="h_grouped", align_bytes=64
+                )
+            nc.vector.scalar_tensor_tensor(
+                out=h_grouped[c][:, j * P * PACK : (j + 1) * P * PACK].rearrange(
+                    "q (r k) -> q r k", k=PACK
+                ),
+                in0=bank[:].rearrange("q (k r) -> q r k", k=PACK),
+                scalar=SQRT_HALF,
+                in1=te_scaled[c][:, :, j * P : (j + 1) * P].rearrange("q k r -> q r k"),
+                op0=ALU.mult,
+                op1=ALU.add,
+            )
+
+        def quantise_h(c):
+            h_codes[c] = two.tile([P, CHUNK], U32, name="h_codes", tag="h_codes", align_bytes=64)
+            h_scales[c] = two.tile([P, CHUNK], U8, name="h_scales", tag="h_scales", align_bytes=64)
+            nc.vector.quantize_mx(
+                out=h_codes[c][:].bitcast(FP8X4), scales=h_scales[c][:], in_=h_grouped[c][:]
+            )
+
+        def second_product(c, j):
+            block = slice(j * P, (j + 1) * P)
+            n = c // CHUNKS_PER_ITEM
+            cols = slice(n * TS, (n + 1) * TS)
+            bank = psum.tile([P, TS], F32, name="scores", tag="scores")
+            nc.tensor.matmul_mx(
+                out=bank[:],
+                lhsT=h_codes[c][:, block].bitcast(FP8X4),
+                lhsT_scale=h_scales[c][:, block],
+                rhs=key_codes[:, cols].bitcast(FP8X4),
+                rhs_scale=key_scales[:, cols],
+                start=True,
+                stop=True,
+            )
+            if j == 0:
+                out_sb[c] = three.tile([P, BLOCKS * TS], F32, name="out_sb", tag="out_sb")
+            nc.scalar.copy(out=out_sb[c][:, j * TS : (j + 1) * TS], in_=bank[:])
+
+        v_sb = keep.tile([P, PACK * C], BF16)
+        nc.sync.dma_start(
+            out=v_sb[:].rearrange("m (half f) -> m half f", half=2),
+            in_=in_proj_v.rearrange("(half m par) c -> m half (par c)", half=2, par=2),
+        )
+        g_sb = keep.tile([P, PACK], BF16)
+        b_sb = keep.tile([P, PACK], BF16)
+        with nc.allow_non_contiguous_dma(reason="gain and bias: two pairs of elements a partition"):
+            nc.scalar.dma_start(
+                out=g_sb[:].rearrange("m (half par) -> m half par", half=2),
+                in_=in_proj_g.rearrange("(half m par) -> m half par", half=2, par=2),
+            )
+            nc.scalar.dma_start(
+                out=b_sb[:].rearrange("m (half par) -> m half par", half=2),
+                in_=in_proj_b.rearrange("(half m par) -> m half par", half=2, par=2),
+            )
+        load_chunk(0)
+        load_keys(0)
+        for c in range(1, LOAD_AHEAD - X_AHEAD):
+            load_chunk(c)
+
+        ident_f32 = keep.tile([P, P], F32)
+        make_identity(nc, ident_f32[:])
+        ident_bf16 = keep.tile([P, P], BF16)
+        make_identity(nc, ident_bf16[:])
+
+        squares = keep.tile([P, PACK * C], BF16)
+        sum_squares = keep.tile([P, PACK], F32)
+        for k in range(PACK):
+            nc.scalar.activation(
+                out=squares[:, k * C : (k + 1) * C],
+                in_=v_sb[:, k * C : (k + 1) * C],
+                func=ACT.Square,
+                accum_out=sum_squares[:, k : k + 1],
+            )
+        norm = keep.tile([P, PACK], F32)
+        nc.scalar.sqrt(out=norm[:], in_=sum_squares[:])
+        inv_norm = keep.tile([P, PACK], F32)
+        nc.vector.reciprocal(out=inv_norm[:], in_=norm[:])
+        gain = keep.tile([P, PACK], F32)
+        nc.vector.tensor_tensor(out=gain[:], in0=inv_norm[:], in1=g_sb[:], op=ALU.mult)
+        bias_scaled = keep.tile([P, PACK], F32)
+        nc.vector.tensor_scalar_mul(out=bias_scaled[:], in0=b_sb[:], scalar1=SQRT_HALF)
+
+        w_sorted = keep.tile([P, PACK * C], BF16)
+        for k in range(PACK):
+            nc.vector.tensor_scalar_mul(
+                out=w_sorted[:, k * C : (k + 1) * C].rearrange(
+                    "m (half par q) -> m half par q", half=2, par=2
+                ),
+                in0=v_sb[:, k * C : (k + 1) * C].rearrange(
+                    "m (half q par) -> m half par q", half=2, par=2
+                ),
+                scalar1=gain[:, k : k + 1],
+            )
+        w_grouped = keep.tile([P, PACK * P * PACK], BF16, align_bytes=64)
+        for a in range(2):
+            bank = psum.tile([P, 2 * PACK * P], BF16, name="wT", tag="hT")
+            for i in range(2 * PACK):
+                nc.tensor.transpose(
+                    bank[:, i * P : (i + 1) * P],
+                    w_sorted[:, (a * 2 * PACK + i) * P : (a * 2 * PACK + i + 1) * P],
+                    ident_bf16[:],
+                )
+            copy_out = nc.vector.tensor_copy if a == 0 else nc.scalar.copy
+            copy_out(
+                out=w_grouped[:, a * 2 * C : (a + 1) * 2 * C].rearrange(
+                    "q (g m k) -> q g m k", g=2, k=PACK
+                ),
+                in_=bank[:].rearrange("q (g k m) -> q g m k", g=2, k=PACK),
+            )
+        w_codes = keep.tile([P, PACK * P], U32, align_bytes=64)
+        w_scales = keep.tile([P, PACK * P], U8, align_bytes=64)
+        nc.vector.quantize_mx(
+            out=w_codes[:].bitcast(FP8X4), scales=w_scales[:], in_=w_grouped[:]
+        )
+
+        for s in range(-X_AHEAD, CHUNKS):
+            c_x, c_te, c_h = s + X_AHEAD, s + TE_AHEAD, s + H_AHEAD
+            h_banks, x_banks, te_banks = {}, {}, {}
+
+            if live(c_h):
+                for j in (0, 1):
+                    h_banks[j] = first_product(c_h, j)
+            if live(c_x):
+                for pair in range(2):
+                    x_banks[pair] = transpose_x(c_x, pair)
+            if live(c_te):
+                for half in range(2):
+                    te_banks[half] = transpose_te(c_te, half)
+            if live(s + LOAD_AHEAD):
+                load_chunk(s + LOAD_AHEAD)
+            if (s + LOAD_AHEAD - 1) % CHUNKS_PER_ITEM == 0 and live(s + LOAD_AHEAD - 1):
+                load_keys((s + LOAD_AHEAD - 1) // CHUNKS_PER_ITEM)
+
+            for first in (0, 2):
+                if live(c_h):
+                    if first == 2:
+                        for j in (2, 3):
+                            h_banks[j] = first_product(c_h, j)
+                    for j in (first, first + 1):
+                        form_h(c_h, j, h_banks[j])
+                if live(c_x):
+                    regroup_x(c_x, first // 2, x_banks[first // 2])
+                if live(c_te):
+                    scale_te(c_te, first // 2, te_banks[first // 2])
+                if live(s):
+                    for j in (first, first + 1):
+                        second_product(s, j)
+            if live(s):
+                store_chunk(s)
+
+            new_keys = live(c_h) and c_h % CHUNKS_PER_ITEM == 0
+            if new_keys:
+                regroup_keys(c_h // CHUNKS_PER_ITEM)
+            if live(c_x):
+                quantise_x(c_x)
+            if live(c_h):
+                quantise_h(c_h)
+            if new_keys:
+                quantise_keys(c_h // CHUNKS_PER_ITEM)

@@ -21,12 +21,11 @@ CHUNKS = BATCH * TQ // CHUNK
 CHUNKS_PER_ITEM = TQ // CHUNK
 SQRT_HALF = math.sqrt(0.5)
 
-X_AHEAD = 3
-TE_AHEAD = 2
+T_AHEAD = 3
+XQ_AHEAD = 2
 H_AHEAD = 1
 LOAD_AHEAD = 8
-X_BUFS = LOAD_AHEAD - X_AHEAD
-TE_BUFS = LOAD_AHEAD - TE_AHEAD
+IN_BUFS = LOAD_AHEAD - T_AHEAD
 
 FLOPS = 2 * BATCH * TQ * C * E + 2 * BATCH * TQ * E * TS
 
@@ -43,16 +42,16 @@ def tile_attentionlayer_pa_t_kernel(
         ctx.enter_context(tc.manual_schedule())
 
         keep = ctx.enter_context(tc.tile_pool(name="keep", bufs=1))
-        x_pool = ctx.enter_context(tc.tile_pool(name="x_pool", bufs=X_BUFS))
-        te_pool = ctx.enter_context(tc.tile_pool(name="te_pool", bufs=TE_BUFS))
+        x_pool = ctx.enter_context(tc.tile_pool(name="x_pool", bufs=IN_BUFS))
+        te_pool = ctx.enter_context(tc.tile_pool(name="te_pool", bufs=IN_BUFS))
         key_pool = ctx.enter_context(tc.tile_pool(name="key_pool", bufs=2))
         two = ctx.enter_context(tc.tile_pool(name="two", bufs=2))
         three = ctx.enter_context(tc.tile_pool(name="three", bufs=3))
-        psum = ctx.enter_context(tc.psum_pool(name="psum", bufs=2))
+        psum = ctx.enter_context(tc.psum_pool(name="psum", bufs=8))
 
         x_in, te_in, key_in = {}, {}, {}
         x_grouped, x_codes, x_scales = {}, {}, {}
-        te_scaled = {}
+        te_T, te_scaled = {}, {}
         h_grouped, h_codes, h_scales = {}, {}, {}
         out_sb = {}
 
@@ -61,13 +60,13 @@ def tile_attentionlayer_pa_t_kernel(
 
         def load_chunk(c):
             rows = slice(c * CHUNK, (c + 1) * CHUNK)
-            x_in[c] = x_pool.tile([P, BLOCKS * C], BF16, name="x_in", tag="x_in")
-            nc.sync.dma_start(
-                out=x_in[c][:], in_=x_rows[rows, :].rearrange("(p j) c -> p (j c)", j=BLOCKS)
-            )
             te_in[c] = te_pool.tile([P, BLOCKS * E], BF16, name="te_in", tag="te_in")
             nc.sync.dma_start(
                 out=te_in[c][:], in_=te_rows[rows, :].rearrange("(p j) e -> p (j e)", j=BLOCKS)
+            )
+            x_in[c] = x_pool.tile([P, BLOCKS * C], BF16, name="x_in", tag="x_in")
+            nc.sync.dma_start(
+                out=x_in[c][:], in_=x_rows[rows, :].rearrange("(p j) c -> p (j c)", j=BLOCKS)
             )
 
         def load_keys(n):
@@ -77,10 +76,12 @@ def tile_attentionlayer_pa_t_kernel(
                 in_=encoder_keys[n].rearrange("(half q par) s -> q half (par s)", half=2, par=2),
             )
 
-        def store_chunk(c):
+        def store_blocks(c, first):
             rows = slice(c * CHUNK, (c + 1) * CHUNK)
+            cols = slice(first * TS, (first + 2) * TS)
             nc.sync.dma_start(
-                out=out_rows[rows, :].rearrange("(p j) s -> p (j s)", j=BLOCKS), in_=out_sb[c][:]
+                out=out_rows[rows, :].rearrange("(p j) s -> p (j s)", j=BLOCKS)[:, cols],
+                in_=out_sb[c][:, cols],
             )
 
         key_codes = keep.tile([P, BATCH * TS], U32, align_bytes=64)
@@ -106,7 +107,7 @@ def tile_attentionlayer_pa_t_kernel(
 
         def transpose_x(c, pair):
             x_words = x_in[c][:].bitcast(F32)
-            bank = psum.tile([P, 4 * P], F32, name="xT", tag="xT")
+            bank = psum.tile([P, 4 * P], F32, name="xT", tag="bank")
             for b in range(2):
                 for half in range(2):
                     word0 = (2 * pair + b) * (C // 2) + half * P
@@ -123,7 +124,8 @@ def tile_attentionlayer_pa_t_kernel(
                     [P, CHUNK * PACK], BF16, name="x_grouped", tag="x_grouped", align_bytes=64
                 )
             words = x_grouped[c][:].bitcast(F32)
-            nc.vector.tensor_copy(
+            copy_out = nc.vector.tensor_copy if pair == 0 else nc.scalar.copy
+            copy_out(
                 out=words[:, pair * 4 * P : (pair + 1) * 4 * P].rearrange(
                     "q (r half) -> q r half", half=2
                 ),
@@ -139,7 +141,7 @@ def tile_attentionlayer_pa_t_kernel(
 
         def transpose_te(c, half):
             te_words = te_in[c][:].bitcast(F32)
-            bank = psum.tile([P, CHUNK], F32, name="teT", tag="teT")
+            bank = psum.tile([P, CHUNK], F32, name="teT", tag="bank")
             for j in range(BLOCKS):
                 word0 = j * (E // 2) + half * P
                 nc.tensor.transpose(
@@ -147,23 +149,29 @@ def tile_attentionlayer_pa_t_kernel(
                 )
             return bank
 
-        def scale_te(c, half, bank):
+        def copy_te(c, half, bank):
             if half == 0:
-                te_scaled[c] = two.tile([P, PACK, CHUNK], F32, name="te_scaled", tag="te_scaled")
-            pairs = bank[:].bitcast(BF16).rearrange("q (r par) -> q r par", par=2)
-            for par in range(2):
-                k = 2 * half + par
-                nc.scalar.activation(
+                te_T[c] = two.tile([P, 2 * CHUNK], F32, name="te_T", tag="te_T")
+            nc.scalar.copy(out=te_T[c][:, half * CHUNK : (half + 1) * CHUNK], in_=bank[:])
+
+        def scale_te(c):
+            te_scaled[c] = three.tile([P, PACK, CHUNK], F32, name="te_scaled", tag="te_scaled")
+            pairs = te_T[c][:].bitcast(BF16).rearrange(
+                "q (half r par) -> q half r par", half=2, par=2
+            )
+            for k in range(PACK):
+                nc.gpsimd.tensor_scalar(
                     out=te_scaled[c][:, k, :],
-                    in_=pairs[:, :, par],
-                    func=ACT.Identity,
-                    bias=bias_scaled[:, k : k + 1],
-                    scale=SQRT_HALF,
+                    in0=pairs[:, k // 2, :, k % 2],
+                    scalar1=SQRT_HALF,
+                    scalar2=bias_scaled[:, k : k + 1],
+                    op0=ALU.mult,
+                    op1=ALU.add,
                 )
 
         def first_product(c, j):
             block = slice(j * P, (j + 1) * P)
-            bank = psum.tile([P, PACK * P], F32, name="hT", tag="hT")
+            bank = psum.tile([P, PACK * P], F32, name="hT", tag="bank")
             for k in range(PACK):
                 group = slice(k * P, (k + 1) * P)
                 nc.tensor.matmul_mx(
@@ -204,7 +212,7 @@ def tile_attentionlayer_pa_t_kernel(
             block = slice(j * P, (j + 1) * P)
             n = c // CHUNKS_PER_ITEM
             cols = slice(n * TS, (n + 1) * TS)
-            bank = psum.tile([P, TS], F32, name="scores", tag="scores")
+            bank = psum.tile([P, TS], F32, name="scores", tag="bank")
             nc.tensor.matmul_mx(
                 out=bank[:],
                 lhsT=h_codes[c][:, block].bitcast(FP8X4),
@@ -217,6 +225,51 @@ def tile_attentionlayer_pa_t_kernel(
             if j == 0:
                 out_sb[c] = three.tile([P, BLOCKS * TS], F32, name="out_sb", tag="out_sb")
             nc.scalar.copy(out=out_sb[c][:, j * TS : (j + 1) * TS], in_=bank[:])
+
+        def pipeline_step(s):
+            c_t, c_xq, c_h = s + T_AHEAD, s + XQ_AHEAD, s + H_AHEAD
+            h_banks, x_banks, te_banks = {}, {}, {}
+            new_keys = live(c_h) and c_h % CHUNKS_PER_ITEM == 0
+
+            if live(c_xq):
+                quantise_x(c_xq)
+            if live(c_h):
+                for j in (0, 1):
+                    h_banks[j] = first_product(c_h, j)
+            if live(c_t):
+                for half in range(2):
+                    te_banks[half] = transpose_te(c_t, half)
+                for pair in range(2):
+                    x_banks[pair] = transpose_x(c_t, pair)
+                for half in range(2):
+                    copy_te(c_t, half, te_banks[half])
+                scale_te(c_t)
+            if live(s + LOAD_AHEAD):
+                load_chunk(s + LOAD_AHEAD)
+            if (s + LOAD_AHEAD - 1) % CHUNKS_PER_ITEM == 0 and live(s + LOAD_AHEAD - 1):
+                load_keys((s + LOAD_AHEAD - 1) // CHUNKS_PER_ITEM)
+
+            for first in (0, 2):
+                if live(c_h):
+                    if first == 2:
+                        for j in (2, 3):
+                            h_banks[j] = first_product(c_h, j)
+                    for j in (first, first + 1):
+                        form_h(c_h, j, h_banks[j])
+                if live(c_t) and first == 2:
+                    for pair in range(2):
+                        regroup_x(c_t, pair, x_banks[pair])
+                if live(s):
+                    for j in (first, first + 1):
+                        second_product(s, j)
+                    store_blocks(s, first)
+
+            if new_keys:
+                regroup_keys(c_h // CHUNKS_PER_ITEM)
+            if live(c_h):
+                quantise_h(c_h)
+            if new_keys:
+                quantise_keys(c_h // CHUNKS_PER_ITEM)
 
         v_sb = keep.tile([P, PACK * C], BF16)
         nc.sync.dma_start(
@@ -236,7 +289,7 @@ def tile_attentionlayer_pa_t_kernel(
             )
         load_chunk(0)
         load_keys(0)
-        for c in range(1, LOAD_AHEAD - X_AHEAD):
+        for c in range(1, IN_BUFS):
             load_chunk(c)
 
         ident_f32 = keep.tile([P, P], F32)
@@ -244,6 +297,11 @@ def tile_attentionlayer_pa_t_kernel(
         ident_bf16 = keep.tile([P, P], BF16)
         make_identity(nc, ident_bf16[:])
 
+        bias_scaled = keep.tile([P, PACK], F32)
+        nc.vector.tensor_scalar_mul(out=bias_scaled[:], in0=b_sb[:], scalar1=SQRT_HALF)
+        one = keep.tile([P, 1], F32)
+        nc.vector.memset(one[:], 1.0)
+        nc.scalar.sqrt(out=one[:], in_=one[:])
         squares = keep.tile([P, PACK * C], BF16)
         sum_squares = keep.tile([P, PACK], F32)
         for k in range(PACK):
@@ -255,12 +313,13 @@ def tile_attentionlayer_pa_t_kernel(
             )
         norm = keep.tile([P, PACK], F32)
         nc.scalar.sqrt(out=norm[:], in_=sum_squares[:])
+
+        pipeline_step(-T_AHEAD)
+
         inv_norm = keep.tile([P, PACK], F32)
         nc.vector.reciprocal(out=inv_norm[:], in_=norm[:])
         gain = keep.tile([P, PACK], F32)
         nc.vector.tensor_tensor(out=gain[:], in0=inv_norm[:], in1=g_sb[:], op=ALU.mult)
-        bias_scaled = keep.tile([P, PACK], F32)
-        nc.vector.tensor_scalar_mul(out=bias_scaled[:], in0=b_sb[:], scalar1=SQRT_HALF)
 
         w_sorted = keep.tile([P, PACK * C], BF16)
         for k in range(PACK):
@@ -275,7 +334,7 @@ def tile_attentionlayer_pa_t_kernel(
             )
         w_grouped = keep.tile([P, PACK * P * PACK], BF16, align_bytes=64)
         for a in range(2):
-            bank = psum.tile([P, 2 * PACK * P], BF16, name="wT", tag="hT")
+            bank = psum.tile([P, 2 * PACK * P], BF16, name="wT", tag="bank")
             for i in range(2 * PACK):
                 nc.tensor.transpose(
                     bank[:, i * P : (i + 1) * P],
@@ -295,47 +354,5 @@ def tile_attentionlayer_pa_t_kernel(
             out=w_codes[:].bitcast(FP8X4), scales=w_scales[:], in_=w_grouped[:]
         )
 
-        for s in range(-X_AHEAD, CHUNKS):
-            c_x, c_te, c_h = s + X_AHEAD, s + TE_AHEAD, s + H_AHEAD
-            h_banks, x_banks, te_banks = {}, {}, {}
-
-            if live(c_h):
-                for j in (0, 1):
-                    h_banks[j] = first_product(c_h, j)
-            if live(c_x):
-                for pair in range(2):
-                    x_banks[pair] = transpose_x(c_x, pair)
-            if live(c_te):
-                for half in range(2):
-                    te_banks[half] = transpose_te(c_te, half)
-            if live(s + LOAD_AHEAD):
-                load_chunk(s + LOAD_AHEAD)
-            if (s + LOAD_AHEAD - 1) % CHUNKS_PER_ITEM == 0 and live(s + LOAD_AHEAD - 1):
-                load_keys((s + LOAD_AHEAD - 1) // CHUNKS_PER_ITEM)
-
-            for first in (0, 2):
-                if live(c_h):
-                    if first == 2:
-                        for j in (2, 3):
-                            h_banks[j] = first_product(c_h, j)
-                    for j in (first, first + 1):
-                        form_h(c_h, j, h_banks[j])
-                if live(c_x):
-                    regroup_x(c_x, first // 2, x_banks[first // 2])
-                if live(c_te):
-                    scale_te(c_te, first // 2, te_banks[first // 2])
-                if live(s):
-                    for j in (first, first + 1):
-                        second_product(s, j)
-            if live(s):
-                store_chunk(s)
-
-            new_keys = live(c_h) and c_h % CHUNKS_PER_ITEM == 0
-            if new_keys:
-                regroup_keys(c_h // CHUNKS_PER_ITEM)
-            if live(c_x):
-                quantise_x(c_x)
-            if live(c_h):
-                quantise_h(c_h)
-            if new_keys:
-                quantise_keys(c_h // CHUNKS_PER_ITEM)
+        for s in range(1 - T_AHEAD, CHUNKS):
+            pipeline_step(s)

@@ -92,9 +92,13 @@ def tile_attentionlayer_pa_t_kernel(
             key_grouped[n] = key_pool.tile(
                 [P, TS * PACK], BF16, name="key_grouped", tag="key_grouped", align_bytes=64
             )
-            nc.vector.tensor_copy(
-                out=key_grouped[n][:].rearrange("q (c i k) -> q c k i", i=4, k=PACK),
-                in_=key_in[n][:].rearrange("q (k c i) -> q c k i", k=PACK, i=4),
+            nc.gpsimd.tensor_scalar(
+                out=key_grouped[n][:].rearrange("q (s k) -> q s k", k=PACK),
+                in0=key_in[n][:].rearrange("q (k s) -> q s k", k=PACK),
+                scalar1=1.0,
+                scalar2=0.0,
+                op0=ALU.mult,
+                op1=ALU.add,
             )
 
         def quantise_keys(n):
@@ -229,12 +233,13 @@ def tile_attentionlayer_pa_t_kernel(
         def pipeline_step(s):
             c_t, c_xq, c_h = s + T_AHEAD, s + XQ_AHEAD, s + H_AHEAD
             h_banks, x_banks, te_banks = {}, {}, {}
-            new_keys = live(c_h) and c_h % CHUNKS_PER_ITEM == 0
+            regroup_item = live(c_xq) and c_xq % CHUNKS_PER_ITEM == 0
+            quantise_item = live(c_h) and c_h % CHUNKS_PER_ITEM == 0
 
             if live(c_xq):
                 quantise_x(c_xq)
             if live(c_h):
-                for j in (0, 1):
+                for j in range(BLOCKS):
                     h_banks[j] = first_product(c_h, j)
             if live(c_t):
                 for half in range(2):
@@ -244,32 +249,29 @@ def tile_attentionlayer_pa_t_kernel(
                 for half in range(2):
                     copy_te(c_t, half, te_banks[half])
                 scale_te(c_t)
+            if regroup_item:
+                regroup_keys(c_xq // CHUNKS_PER_ITEM)
             if live(s + LOAD_AHEAD):
                 load_chunk(s + LOAD_AHEAD)
             if (s + LOAD_AHEAD - 1) % CHUNKS_PER_ITEM == 0 and live(s + LOAD_AHEAD - 1):
                 load_keys((s + LOAD_AHEAD - 1) // CHUNKS_PER_ITEM)
 
-            for first in (0, 2):
-                if live(c_h):
-                    if first == 2:
-                        for j in (2, 3):
-                            h_banks[j] = first_product(c_h, j)
-                    for j in (first, first + 1):
-                        form_h(c_h, j, h_banks[j])
-                if live(c_t) and first == 2:
-                    for pair in range(2):
-                        regroup_x(c_t, pair, x_banks[pair])
-                if live(s):
-                    for j in (first, first + 1):
-                        second_product(s, j)
-                    store_blocks(s, first)
-
-            if new_keys:
-                regroup_keys(c_h // CHUNKS_PER_ITEM)
+            if live(c_h):
+                for j in range(BLOCKS):
+                    form_h(c_h, j, h_banks[j])
+            if live(c_t):
+                for pair in range(2):
+                    regroup_x(c_t, pair, x_banks[pair])
             if live(c_h):
                 quantise_h(c_h)
-            if new_keys:
+            if quantise_item:
                 quantise_keys(c_h // CHUNKS_PER_ITEM)
+
+            if live(s):
+                for j in range(BLOCKS):
+                    second_product(s, j)
+                    if j % 2 == 1:
+                        store_blocks(s, j - 1)
 
         v_sb = keep.tile([P, PACK * C], BF16)
         nc.sync.dma_start(

@@ -236,16 +236,17 @@ def tile_attentionlayer_pa_t_kernel(
             regroup_item = live(c_xq) and c_xq % CHUNKS_PER_ITEM == 0
             quantise_item = live(c_h) and c_h % CHUNKS_PER_ITEM == 0
 
-            if live(c_xq):
-                quantise_x(c_xq)
+            if live(c_t):
+                for pair in range(2):
+                    x_banks[pair] = transpose_x(c_t, pair)
+                for pair in range(2):
+                    regroup_x(c_t, pair, x_banks[pair])
             if live(c_h):
                 for j in range(BLOCKS):
                     h_banks[j] = first_product(c_h, j)
             if live(c_t):
                 for half in range(2):
                     te_banks[half] = transpose_te(c_t, half)
-                for pair in range(2):
-                    x_banks[pair] = transpose_x(c_t, pair)
                 for half in range(2):
                     copy_te(c_t, half, te_banks[half])
                 scale_te(c_t)
@@ -259,9 +260,8 @@ def tile_attentionlayer_pa_t_kernel(
             if live(c_h):
                 for j in range(BLOCKS):
                     form_h(c_h, j, h_banks[j])
-            if live(c_t):
-                for pair in range(2):
-                    regroup_x(c_t, pair, x_banks[pair])
+            if live(c_xq):
+                quantise_x(c_xq)
             if live(c_h):
                 quantise_h(c_h)
             if quantise_item:

@@ -51,7 +51,7 @@ def tile_attentionlayer_pa_t_kernel(
 
         x_in, te_in, key_in = {}, {}, {}
         x_grouped, x_codes, x_scales = {}, {}, {}
-        te_T, te_scaled = {}, {}
+        te_scaled = {}
         h_grouped, h_codes, h_scales = {}, {}, {}
         out_sb = {}
 
@@ -128,8 +128,7 @@ def tile_attentionlayer_pa_t_kernel(
                     [P, CHUNK * PACK], BF16, name="x_grouped", tag="x_grouped", align_bytes=64
                 )
             words = x_grouped[c][:].bitcast(F32)
-            copy_out = nc.vector.tensor_copy if pair == 0 else nc.scalar.copy
-            copy_out(
+            nc.vector.tensor_copy(
                 out=words[:, pair * 4 * P : (pair + 1) * 4 * P].rearrange(
                     "q (r half) -> q r half", half=2
                 ),
@@ -153,24 +152,18 @@ def tile_attentionlayer_pa_t_kernel(
                 )
             return bank
 
-        def copy_te(c, half, bank):
+        def scale_te(c, half, bank):
             if half == 0:
-                te_T[c] = two.tile([P, 2 * CHUNK], F32, name="te_T", tag="te_T")
-            nc.scalar.copy(out=te_T[c][:, half * CHUNK : (half + 1) * CHUNK], in_=bank[:])
-
-        def scale_te(c):
-            te_scaled[c] = three.tile([P, PACK, CHUNK], F32, name="te_scaled", tag="te_scaled")
-            pairs = te_T[c][:].bitcast(BF16).rearrange(
-                "q (half r par) -> q half r par", half=2, par=2
-            )
-            for k in range(PACK):
-                nc.gpsimd.tensor_scalar(
+                te_scaled[c] = three.tile([P, PACK, CHUNK], F32, name="te_scaled", tag="te_scaled")
+            pairs = bank[:].bitcast(BF16).rearrange("q (r par) -> q r par", par=2)
+            for par in range(2):
+                k = 2 * half + par
+                nc.scalar.activation(
                     out=te_scaled[c][:, k, :],
-                    in0=pairs[:, k // 2, :, k % 2],
-                    scalar1=SQRT_HALF,
-                    scalar2=bias_scaled[:, k : k + 1],
-                    op0=ALU.mult,
-                    op1=ALU.add,
+                    in_=pairs[:, :, par],
+                    func=ACT.Identity,
+                    bias=bias_scaled[:, k : k + 1],
+                    scale=SQRT_HALF,
                 )
 
         def first_product(c, j):
@@ -236,20 +229,18 @@ def tile_attentionlayer_pa_t_kernel(
             regroup_item = live(c_xq) and c_xq % CHUNKS_PER_ITEM == 0
             quantise_item = live(c_h) and c_h % CHUNKS_PER_ITEM == 0
 
-            if live(c_t):
-                for pair in range(2):
-                    x_banks[pair] = transpose_x(c_t, pair)
-                for pair in range(2):
-                    regroup_x(c_t, pair, x_banks[pair])
+            if live(c_xq):
+                quantise_x(c_xq)
             if live(c_h):
                 for j in range(BLOCKS):
                     h_banks[j] = first_product(c_h, j)
             if live(c_t):
                 for half in range(2):
                     te_banks[half] = transpose_te(c_t, half)
+                for pair in range(2):
+                    x_banks[pair] = transpose_x(c_t, pair)
                 for half in range(2):
-                    copy_te(c_t, half, te_banks[half])
-                scale_te(c_t)
+                    scale_te(c_t, half, te_banks[half])
             if regroup_item:
                 regroup_keys(c_xq // CHUNKS_PER_ITEM)
             if live(s + LOAD_AHEAD):
@@ -260,8 +251,9 @@ def tile_attentionlayer_pa_t_kernel(
             if live(c_h):
                 for j in range(BLOCKS):
                     form_h(c_h, j, h_banks[j])
-            if live(c_xq):
-                quantise_x(c_xq)
+            if live(c_t):
+                for pair in range(2):
+                    regroup_x(c_t, pair, x_banks[pair])
             if live(c_h):
                 quantise_h(c_h)
             if quantise_item:

@@ -51,7 +51,7 @@ def tile_attentionlayer_pa_t_kernel(
 
         x_in, te_in, key_in = {}, {}, {}
         x_grouped, x_codes, x_scales = {}, {}, {}
-        te_scaled = {}
+        te_T, te_scaled = {}, {}
         h_grouped, h_codes, h_scales = {}, {}, {}
         out_sb = {}
 
@@ -92,13 +92,9 @@ def tile_attentionlayer_pa_t_kernel(
             key_grouped[n] = key_pool.tile(
                 [P, TS * PACK], BF16, name="key_grouped", tag="key_grouped", align_bytes=64
             )
-            nc.gpsimd.tensor_scalar(
-                out=key_grouped[n][:].rearrange("q (s k) -> q s k", k=PACK),
-                in0=key_in[n][:].rearrange("q (k s) -> q s k", k=PACK),
-                scalar1=1.0,
-                scalar2=0.0,
-                op0=ALU.mult,
-                op1=ALU.add,
+            nc.vector.tensor_copy(
+                out=key_grouped[n][:].rearrange("q (c i k) -> q c k i", i=4, k=PACK),
+                in_=key_in[n][:].rearrange("q (k c i) -> q c k i", k=PACK, i=4),
             )
 
         def quantise_keys(n):
@@ -128,7 +124,7 @@ def tile_attentionlayer_pa_t_kernel(
                     [P, CHUNK * PACK], BF16, name="x_grouped", tag="x_grouped", align_bytes=64
                 )
             words = x_grouped[c][:].bitcast(F32)
-            nc.vector.tensor_copy(
+            nc.scalar.copy(
                 out=words[:, pair * 4 * P : (pair + 1) * 4 * P].rearrange(
                     "q (r half) -> q r half", half=2
                 ),
@@ -152,18 +148,24 @@ def tile_attentionlayer_pa_t_kernel(
                 )
             return bank
 
-        def scale_te(c, half, bank):
+        def copy_te(c, half, bank):
             if half == 0:
-                te_scaled[c] = three.tile([P, PACK, CHUNK], F32, name="te_scaled", tag="te_scaled")
-            pairs = bank[:].bitcast(BF16).rearrange("q (r par) -> q r par", par=2)
-            for par in range(2):
-                k = 2 * half + par
-                nc.scalar.activation(
+                te_T[c] = two.tile([P, 2 * CHUNK], F32, name="te_T", tag="te_T")
+            nc.scalar.copy(out=te_T[c][:, half * CHUNK : (half + 1) * CHUNK], in_=bank[:])
+
+        def scale_te(c):
+            te_scaled[c] = three.tile([P, PACK, CHUNK], F32, name="te_scaled", tag="te_scaled")
+            pairs = te_T[c][:].bitcast(BF16).rearrange(
+                "q (half r par) -> q half r par", half=2, par=2
+            )
+            for k in range(PACK):
+                nc.gpsimd.tensor_scalar(
                     out=te_scaled[c][:, k, :],
-                    in_=pairs[:, :, par],
-                    func=ACT.Identity,
-                    bias=bias_scaled[:, k : k + 1],
-                    scale=SQRT_HALF,
+                    in0=pairs[:, k // 2, :, k % 2],
+                    scalar1=SQRT_HALF,
+                    scalar2=bias_scaled[:, k : k + 1],
+                    op0=ALU.mult,
+                    op1=ALU.add,
                 )
 
         def first_product(c, j):
@@ -221,16 +223,20 @@ def tile_attentionlayer_pa_t_kernel(
             )
             if j == 0:
                 out_sb[c] = three.tile([P, BLOCKS * TS], F32, name="out_sb", tag="out_sb")
-            nc.scalar.copy(out=out_sb[c][:, j * TS : (j + 1) * TS], in_=bank[:])
+            copy_out = nc.vector.tensor_copy if c == CHUNKS - 1 and j % 2 == 1 else nc.scalar.copy
+            copy_out(out=out_sb[c][:, j * TS : (j + 1) * TS], in_=bank[:])
 
         def pipeline_step(s):
             c_t, c_xq, c_h = s + T_AHEAD, s + XQ_AHEAD, s + H_AHEAD
             h_banks, x_banks, te_banks = {}, {}, {}
-            regroup_item = live(c_xq) and c_xq % CHUNKS_PER_ITEM == 0
-            quantise_item = live(c_h) and c_h % CHUNKS_PER_ITEM == 0
 
             if live(c_xq):
                 quantise_x(c_xq)
+            if live(s):
+                quantise_h(s)
+                if s % CHUNKS_PER_ITEM == 0:
+                    quantise_keys(s // CHUNKS_PER_ITEM)
+
             if live(c_h):
                 for j in range(BLOCKS):
                     h_banks[j] = first_product(c_h, j)
@@ -240,9 +246,10 @@ def tile_attentionlayer_pa_t_kernel(
                 for pair in range(2):
                     x_banks[pair] = transpose_x(c_t, pair)
                 for half in range(2):
-                    scale_te(c_t, half, te_banks[half])
-            if regroup_item:
-                regroup_keys(c_xq // CHUNKS_PER_ITEM)
+                    copy_te(c_t, half, te_banks[half])
+                scale_te(c_t)
+                for pair in range(2):
+                    regroup_x(c_t, pair, x_banks[pair])
             if live(s + LOAD_AHEAD):
                 load_chunk(s + LOAD_AHEAD)
             if (s + LOAD_AHEAD - 1) % CHUNKS_PER_ITEM == 0 and live(s + LOAD_AHEAD - 1):
@@ -251,13 +258,8 @@ def tile_attentionlayer_pa_t_kernel(
             if live(c_h):
                 for j in range(BLOCKS):
                     form_h(c_h, j, h_banks[j])
-            if live(c_t):
-                for pair in range(2):
-                    regroup_x(c_t, pair, x_banks[pair])
-            if live(c_h):
-                quantise_h(c_h)
-            if quantise_item:
-                quantise_keys(c_h // CHUNKS_PER_ITEM)
+                if c_h % CHUNKS_PER_ITEM == 0:
+                    regroup_keys(c_h // CHUNKS_PER_ITEM)
 
             if live(s):
                 for j in range(BLOCKS):

@@ -21,10 +21,11 @@ CHUNKS = BATCH * TQ // CHUNK
 CHUNKS_PER_ITEM = TQ // CHUNK
 SQRT_HALF = math.sqrt(0.5)
 
-T_AHEAD = 3
-XQ_AHEAD = 2
-H_AHEAD = 1
-LOAD_AHEAD = 8
+T_AHEAD = 4
+XQ_AHEAD = 3
+H_AHEAD = 2
+SCALE_AHEAD = 1
+LOAD_AHEAD = 9
 IN_BUFS = LOAD_AHEAD - T_AHEAD
 
 FLOPS = 2 * BATCH * TQ * C * E + 2 * BATCH * TQ * E * TS
@@ -51,8 +52,8 @@ def tile_attentionlayer_pa_t_kernel(
 
         x_in, te_in, key_in = {}, {}, {}
         x_grouped, x_codes, x_scales = {}, {}, {}
-        te_T, te_scaled = {}, {}
-        h_grouped, h_codes, h_scales = {}, {}, {}
+        te_T = {}
+        h_sum, h_grouped, h_codes, h_scales = {}, {}, {}, {}
         out_sb = {}
 
         def live(c):
@@ -150,55 +151,57 @@ def tile_attentionlayer_pa_t_kernel(
 
         def copy_te(c, half, bank):
             if half == 0:
-                te_T[c] = two.tile([P, 2 * CHUNK], F32, name="te_T", tag="te_T")
+                te_T[c] = three.tile([P, 2 * CHUNK], F32, name="te_T", tag="te_T")
             nc.scalar.copy(out=te_T[c][:, half * CHUNK : (half + 1) * CHUNK], in_=bank[:])
 
-        def scale_te(c):
-            te_scaled[c] = three.tile([P, PACK, CHUNK], F32, name="te_scaled", tag="te_scaled")
+        def first_product(c, k):
+            group = slice(k * P, (k + 1) * P)
+            bank = psum.tile([P, CHUNK], F32, name="hT", tag="bank")
+            nc.tensor.matmul_mx(
+                out=bank[:],
+                lhsT=w_codes[:, group].bitcast(FP8X4),
+                lhsT_scale=w_scales[:, group],
+                rhs=x_codes[c][:].bitcast(FP8X4),
+                rhs_scale=x_scales[c][:],
+                start=True,
+                stop=True,
+            )
+            return bank
+
+        def sum_h(c, k, bank):
+            if k == 0:
+                h_sum[c] = two.tile([P, PACK, CHUNK], F32, name="h_sum", tag="h_sum")
             pairs = te_T[c][:].bitcast(BF16).rearrange(
                 "q (half r par) -> q half r par", half=2, par=2
             )
-            for k in range(PACK):
+            nc.vector.scalar_tensor_tensor(
+                out=h_sum[c][:, k, :],
+                in0=bank[:],
+                scalar=bias[:, k : k + 1],
+                in1=pairs[:, k // 2, :, k % 2],
+                op0=ALU.add,
+                op1=ALU.add,
+            )
+
+        def hold_gpsimd(codes):
+            seen = two.tile([P, 1], U32, name="seen", tag="seen")
+            nc.gpsimd.tensor_copy(out=seen[:], in_=codes[:, 0:1])
+
+        def scale_h(c):
+            h_grouped[c] = two.tile(
+                [P, CHUNK * PACK], BF16, name="h_grouped", tag="h_grouped", align_bytes=64
+            )
+            for part in range(2):
+                tokens = slice(part * CHUNK // 2, (part + 1) * CHUNK // 2)
+                values = slice(part * CHUNK // 2 * PACK, (part + 1) * CHUNK // 2 * PACK)
                 nc.gpsimd.tensor_scalar(
-                    out=te_scaled[c][:, k, :],
-                    in0=pairs[:, k // 2, :, k % 2],
+                    out=h_grouped[c][:, values].rearrange("q (b i k) -> q b k i", i=4, k=PACK),
+                    in0=h_sum[c][:, :, tokens].rearrange("q k (b i) -> q b k i", i=4),
                     scalar1=SQRT_HALF,
-                    scalar2=bias_scaled[:, k : k + 1],
+                    scalar2=0.0,
                     op0=ALU.mult,
                     op1=ALU.add,
                 )
-
-        def first_product(c, j):
-            block = slice(j * P, (j + 1) * P)
-            bank = psum.tile([P, PACK * P], F32, name="hT", tag="bank")
-            for k in range(PACK):
-                group = slice(k * P, (k + 1) * P)
-                nc.tensor.matmul_mx(
-                    out=bank[:, group],
-                    lhsT=w_codes[:, group].bitcast(FP8X4),
-                    lhsT_scale=w_scales[:, group],
-                    rhs=x_codes[c][:, block].bitcast(FP8X4),
-                    rhs_scale=x_scales[c][:, block],
-                    start=True,
-                    stop=True,
-                )
-            return bank
-
-        def form_h(c, j, bank):
-            if j == 0:
-                h_grouped[c] = two.tile(
-                    [P, CHUNK * PACK], BF16, name="h_grouped", tag="h_grouped", align_bytes=64
-                )
-            nc.vector.scalar_tensor_tensor(
-                out=h_grouped[c][:, j * P * PACK : (j + 1) * P * PACK].rearrange(
-                    "q (r k) -> q r k", k=PACK
-                ),
-                in0=bank[:].rearrange("q (k r) -> q r k", k=PACK),
-                scalar=SQRT_HALF,
-                in1=te_scaled[c][:, :, j * P : (j + 1) * P].rearrange("q k r -> q r k"),
-                op0=ALU.mult,
-                op1=ALU.add,
-            )
 
         def quantise_h(c):
             h_codes[c] = two.tile([P, CHUNK], U32, name="h_codes", tag="h_codes", align_bytes=64)
@@ -227,19 +230,26 @@ def tile_attentionlayer_pa_t_kernel(
             copy_out(out=out_sb[c][:, j * TS : (j + 1) * TS], in_=bank[:])
 
         def pipeline_step(s):
-            c_t, c_xq, c_h = s + T_AHEAD, s + XQ_AHEAD, s + H_AHEAD
+            c_t, c_xq, c_h, c_g = s + T_AHEAD, s + XQ_AHEAD, s + H_AHEAD, s + SCALE_AHEAD
             h_banks, x_banks, te_banks = {}, {}, {}
 
+            last_codes = None
             if live(c_xq):
                 quantise_x(c_xq)
+                last_codes = x_codes[c_xq]
             if live(s):
                 quantise_h(s)
+                last_codes = h_codes[s]
                 if s % CHUNKS_PER_ITEM == 0:
                     quantise_keys(s // CHUNKS_PER_ITEM)
+            if live(c_g):
+                if last_codes is not None:
+                    hold_gpsimd(last_codes)
+                scale_h(c_g)
 
             if live(c_h):
-                for j in range(BLOCKS):
-                    h_banks[j] = first_product(c_h, j)
+                for k in range(PACK):
+                    h_banks[k] = first_product(c_h, k)
             if live(c_t):
                 for half in range(2):
                     te_banks[half] = transpose_te(c_t, half)
@@ -247,7 +257,6 @@ def tile_attentionlayer_pa_t_kernel(
                     x_banks[pair] = transpose_x(c_t, pair)
                 for half in range(2):
                     copy_te(c_t, half, te_banks[half])
-                scale_te(c_t)
                 for pair in range(2):
                     regroup_x(c_t, pair, x_banks[pair])
             if live(s + LOAD_AHEAD):
@@ -256,10 +265,10 @@ def tile_attentionlayer_pa_t_kernel(
                 load_keys((s + LOAD_AHEAD - 1) // CHUNKS_PER_ITEM)
 
             if live(c_h):
-                for j in range(BLOCKS):
-                    form_h(c_h, j, h_banks[j])
-                if c_h % CHUNKS_PER_ITEM == 0:
-                    regroup_keys(c_h // CHUNKS_PER_ITEM)
+                for k in range(PACK):
+                    sum_h(c_h, k, h_banks[k])
+            if live(c_g) and c_g % CHUNKS_PER_ITEM == 0:
+                regroup_keys(c_g // CHUNKS_PER_ITEM)
 
             if live(s):
                 for j in range(BLOCKS):
@@ -293,8 +302,8 @@ def tile_attentionlayer_pa_t_kernel(
         ident_bf16 = keep.tile([P, P], BF16)
         make_identity(nc, ident_bf16[:])
 
-        bias_scaled = keep.tile([P, PACK], F32)
-        nc.vector.tensor_scalar_mul(out=bias_scaled[:], in0=b_sb[:], scalar1=SQRT_HALF)
+        bias = keep.tile([P, PACK], F32)
+        nc.vector.tensor_copy(out=bias[:], in_=b_sb[:])
         one = keep.tile([P, 1], F32)
         nc.vector.memset(one[:], 1.0)
         nc.scalar.sqrt(out=one[:], in_=one[:])

@@ -183,25 +183,27 @@ def tile_attentionlayer_pa_t_kernel(
                 op1=ALU.add,
             )
 
-        def hold_gpsimd(codes):
-            seen = two.tile([P, 1], U32, name="seen", tag="seen")
-            nc.gpsimd.tensor_copy(out=seen[:], in_=codes[:, 0:1])
+        def hold_gpsimd(values):
+            seen = two.tile([P, 1], BF16, name="seen", tag="seen")
+            nc.gpsimd.tensor_copy(out=seen[:], in_=values)
 
         def scale_h(c):
             h_grouped[c] = two.tile(
                 [P, CHUNK * PACK], BF16, name="h_grouped", tag="h_grouped", align_bytes=64
             )
-            for part in range(2):
+
+            def half(part):
                 tokens = slice(part * CHUNK // 2, (part + 1) * CHUNK // 2)
                 values = slice(part * CHUNK // 2 * PACK, (part + 1) * CHUNK // 2 * PACK)
-                nc.gpsimd.tensor_scalar(
+                return dict(
                     out=h_grouped[c][:, values].rearrange("q (b i k) -> q b k i", i=4, k=PACK),
                     in0=h_sum[c][:, :, tokens].rearrange("q k (b i) -> q b k i", i=4),
                     scalar1=SQRT_HALF,
-                    scalar2=0.0,
-                    op0=ALU.mult,
-                    op1=ALU.add,
                 )
+
+            nc.vector.tensor_scalar(scalar2=None, op0=ALU.mult, **half(0))
+            hold_gpsimd(h_grouped[c][:, 0:1])
+            nc.gpsimd.tensor_scalar(scalar2=0.0, op0=ALU.mult, op1=ALU.add, **half(1))
 
         def quantise_h(c):
             h_codes[c] = two.tile([P, CHUNK], U32, name="h_codes", tag="h_codes", align_bytes=64)
@@ -233,18 +235,13 @@ def tile_attentionlayer_pa_t_kernel(
             c_t, c_xq, c_h, c_g = s + T_AHEAD, s + XQ_AHEAD, s + H_AHEAD, s + SCALE_AHEAD
             h_banks, x_banks, te_banks = {}, {}, {}
 
-            last_codes = None
             if live(c_xq):
                 quantise_x(c_xq)
-                last_codes = x_codes[c_xq]
             if live(s):
                 quantise_h(s)
-                last_codes = h_codes[s]
                 if s % CHUNKS_PER_ITEM == 0:
                     quantise_keys(s // CHUNKS_PER_ITEM)
             if live(c_g):
-                if last_codes is not None:
-                    hold_gpsimd(last_codes)
                 scale_h(c_g)
 
             if live(c_h):

@@ -23,9 +23,12 @@ SQRT_HALF = math.sqrt(0.5)
 
 T_AHEAD = 4
 XQ_AHEAD = 3
-H_AHEAD = 2
-SCALE_AHEAD = 1
-LOAD_AHEAD = 9
+P_AHEAD = 2
+H_AHEAD = 1
+G_BLOCKS = 1
+LOAD_AHEAD = 10
+KEYS_AHEAD = 8
+KEY_PARTS = 4
 IN_BUFS = LOAD_AHEAD - T_AHEAD
 
 FLOPS = 2 * BATCH * TQ * C * E + 2 * BATCH * TQ * E * TS
@@ -48,7 +51,9 @@ def tile_attentionlayer_pa_t_kernel(
         key_pool = ctx.enter_context(tc.tile_pool(name="key_pool", bufs=2))
         two = ctx.enter_context(tc.tile_pool(name="two", bufs=2))
         three = ctx.enter_context(tc.tile_pool(name="three", bufs=3))
-        psum = ctx.enter_context(tc.psum_pool(name="psum", bufs=8))
+        four = ctx.enter_context(tc.tile_pool(name="four", bufs=4))
+        psum = ctx.enter_context(tc.psum_pool(name="psum", bufs=4))
+        psum_h = ctx.enter_context(tc.psum_pool(name="psum_h", bufs=4))
 
         x_in, te_in, key_in = {}, {}, {}
         x_grouped, x_codes, x_scales = {}, {}, {}
@@ -77,9 +82,9 @@ def tile_attentionlayer_pa_t_kernel(
                 in_=encoder_keys[n].rearrange("(half q par) s -> q half (par s)", half=2, par=2),
             )
 
-        def store_blocks(c, first):
+        def store_blocks(c, first, count):
             rows = slice(c * CHUNK, (c + 1) * CHUNK)
-            cols = slice(first * TS, (first + 2) * TS)
+            cols = slice(first * TS, (first + count) * TS)
             nc.sync.dma_start(
                 out=out_rows[rows, :].rearrange("(p j) s -> p (j s)", j=BLOCKS)[:, cols],
                 in_=out_sb[c][:, cols],
@@ -89,14 +94,29 @@ def tile_attentionlayer_pa_t_kernel(
         key_scales = keep.tile([P, BATCH * TS], U8, align_bytes=64)
         key_grouped = {}
 
-        def regroup_keys(n):
-            key_grouped[n] = key_pool.tile(
-                [P, TS * PACK], BF16, name="key_grouped", tag="key_grouped", align_bytes=64
-            )
-            nc.vector.tensor_copy(
-                out=key_grouped[n][:].rearrange("q (c i k) -> q c k i", i=4, k=PACK),
-                in_=key_in[n][:].rearrange("q (k c i) -> q c k i", k=PACK, i=4),
-            )
+        def regroup_keys(n, part):
+            if not part:
+                key_grouped[n] = key_pool.tile(
+                    [P, TS * PACK], BF16, name="key_grouped", tag="key_grouped", align_bytes=64
+                )
+            keys_out = key_grouped[n][:].rearrange("q (b i k) -> q b k i", i=4, k=PACK)
+            keys_in = key_in[n][:].rearrange("q (k b i) -> q b k i", k=PACK, i=4)
+            if part is None:
+                nc.vector.tensor_copy(out=keys_out, in_=keys_in)
+            else:
+                runs = slice(part * TS // 4 // KEY_PARTS, (part + 1) * TS // 4 // KEY_PARTS)
+                nc.gpsimd.tensor_scalar(
+                    out=keys_out[:, runs],
+                    in0=keys_in[:, runs],
+                    scalar1=1.0,
+                    scalar2=0.0,
+                    op0=ALU.mult,
+                    op1=ALU.add,
+                )
+
+        def hold_gpsimd(codes):
+            seen = two.tile([P, 1], U32, name="seen", tag="seen")
+            nc.gpsimd.tensor_copy(out=seen[:], in_=codes[:, 0:1])
 
         def quantise_keys(n):
             cols = slice(n * TS, (n + 1) * TS)
@@ -121,7 +141,7 @@ def tile_attentionlayer_pa_t_kernel(
 
         def regroup_x(c, pair, bank):
             if pair == 0:
-                x_grouped[c] = two.tile(
+                x_grouped[c] = three.tile(
                     [P, CHUNK * PACK], BF16, name="x_grouped", tag="x_grouped", align_bytes=64
                 )
             words = x_grouped[c][:].bitcast(F32)
@@ -151,12 +171,12 @@ def tile_attentionlayer_pa_t_kernel(
 
         def copy_te(c, half, bank):
             if half == 0:
-                te_T[c] = three.tile([P, 2 * CHUNK], F32, name="te_T", tag="te_T")
+                te_T[c] = four.tile([P, 2 * CHUNK], F32, name="te_T", tag="te_T")
             nc.scalar.copy(out=te_T[c][:, half * CHUNK : (half + 1) * CHUNK], in_=bank[:])
 
         def first_product(c, k):
             group = slice(k * P, (k + 1) * P)
-            bank = psum.tile([P, CHUNK], F32, name="hT", tag="bank")
+            bank = psum_h.tile([P, CHUNK], F32, name="hT", tag="bank_h")
             nc.tensor.matmul_mx(
                 out=bank[:],
                 lhsT=w_codes[:, group].bitcast(FP8X4),
@@ -183,36 +203,49 @@ def tile_attentionlayer_pa_t_kernel(
                 op1=ALU.add,
             )
 
-        def hold_gpsimd(values):
-            seen = two.tile([P, 1], BF16, name="seen", tag="seen")
-            nc.gpsimd.tensor_copy(out=seen[:], in_=values)
+        def shared_with_scalar(c):
+            return not live(c - H_AHEAD + T_AHEAD)
+
+        def scaled(c, first, last):
+            runs = slice(first * P // 4, last * P // 4)
+            return (
+                h_grouped[c][:].rearrange("q (b i k) -> q b k i", i=4, k=PACK)[:, runs],
+                h_sum[c][:].rearrange("q k (b i) -> q b k i", i=4)[:, runs],
+            )
 
         def scale_h(c):
             h_grouped[c] = two.tile(
                 [P, CHUNK * PACK], BF16, name="h_grouped", tag="h_grouped", align_bytes=64
             )
+            blocks = BLOCKS // 2 if shared_with_scalar(c) else BLOCKS - G_BLOCKS
+            h_out, h_in = scaled(c, 0, blocks)
+            nc.vector.tensor_scalar(
+                out=h_out, in0=h_in, scalar1=SQRT_HALF, scalar2=None, op0=ALU.mult
+            )
+            if shared_with_scalar(c):
+                h_out, h_in = scaled(c, blocks, BLOCKS)
+                nc.scalar.activation(out=h_out, in_=h_in, func=ACT.Copy, scale=SQRT_HALF)
 
-            def half(part):
-                tokens = slice(part * CHUNK // 2, (part + 1) * CHUNK // 2)
-                values = slice(part * CHUNK // 2 * PACK, (part + 1) * CHUNK // 2 * PACK)
-                return dict(
-                    out=h_grouped[c][:, values].rearrange("q (b i k) -> q b k i", i=4, k=PACK),
-                    in0=h_sum[c][:, :, tokens].rearrange("q k (b i) -> q b k i", i=4),
-                    scalar1=SQRT_HALF,
-                )
-
-            nc.vector.tensor_scalar(scalar2=None, op0=ALU.mult, **half(0))
-            hold_gpsimd(h_grouped[c][:, 0:1])
-            nc.gpsimd.tensor_scalar(scalar2=0.0, op0=ALU.mult, op1=ALU.add, **half(1))
+        def scale_h_gpsimd(c):
+            h_out, h_in = scaled(c, BLOCKS - G_BLOCKS, BLOCKS)
+            nc.gpsimd.tensor_scalar(
+                out=h_out, in0=h_in, scalar1=SQRT_HALF, scalar2=0.0, op0=ALU.mult, op1=ALU.add
+            )
 
         def quantise_h(c):
             h_codes[c] = two.tile([P, CHUNK], U32, name="h_codes", tag="h_codes", align_bytes=64)
             h_scales[c] = two.tile([P, CHUNK], U8, name="h_scales", tag="h_scales", align_bytes=64)
-            nc.vector.quantize_mx(
-                out=h_codes[c][:].bitcast(FP8X4), scales=h_scales[c][:], in_=h_grouped[c][:]
-            )
+            parts = 2 if c == CHUNKS - 1 else 1
+            for part in range(parts):
+                words = slice(part * CHUNK // parts, (part + 1) * CHUNK // parts)
+                values = slice(part * CHUNK // parts * PACK, (part + 1) * CHUNK // parts * PACK)
+                nc.vector.quantize_mx(
+                    out=h_codes[c][:, words].bitcast(FP8X4),
+                    scales=h_scales[c][:, words],
+                    in_=h_grouped[c][:, values],
+                )
 
-        def second_product(c, j):
+        def second_product(c, j, copy_out):
             block = slice(j * P, (j + 1) * P)
             n = c // CHUNKS_PER_ITEM
             cols = slice(n * TS, (n + 1) * TS)
@@ -228,56 +261,79 @@ def tile_attentionlayer_pa_t_kernel(
             )
             if j == 0:
                 out_sb[c] = three.tile([P, BLOCKS * TS], F32, name="out_sb", tag="out_sb")
-            copy_out = nc.vector.tensor_copy if c == CHUNKS - 1 and j % 2 == 1 else nc.scalar.copy
             copy_out(out=out_sb[c][:, j * TS : (j + 1) * TS], in_=bank[:])
 
-        def pipeline_step(s):
-            c_t, c_xq, c_h, c_g = s + T_AHEAD, s + XQ_AHEAD, s + H_AHEAD, s + SCALE_AHEAD
-            h_banks, x_banks, te_banks = {}, {}, {}
+        h_banks = {}
 
-            if live(c_xq):
-                quantise_x(c_xq)
-            if live(s):
-                quantise_h(s)
-                if s % CHUNKS_PER_ITEM == 0:
-                    quantise_keys(s // CHUNKS_PER_ITEM)
-            if live(c_g):
-                scale_h(c_g)
+        def pipeline_step(s):
+            c_t, c_xq, c_p, c_h = s + T_AHEAD, s + XQ_AHEAD, s + P_AHEAD, s + H_AHEAD
+            x_banks, te_banks = {}, {}
 
             if live(c_h):
                 for k in range(PACK):
-                    h_banks[k] = first_product(c_h, k)
+                    sum_h(c_h, k, h_banks[c_h, k])
+            if c_h == 0:
+                quantise_x(1)
+            if live(s):
+                if live(c_xq - 1):
+                    hold_gpsimd(x_codes[c_xq - 1])
+                if not shared_with_scalar(s):
+                    scale_h_gpsimd(s)
+                n, part = divmod(s, CHUNKS_PER_ITEM)
+                if n + 1 < BATCH:
+                    regroup_keys(n + 1, part)
+
             if live(c_t):
                 for half in range(2):
                     te_banks[half] = transpose_te(c_t, half)
-                for pair in range(2):
-                    x_banks[pair] = transpose_x(c_t, pair)
                 for half in range(2):
                     copy_te(c_t, half, te_banks[half])
+            if live(c_p):
+                for k in range(PACK):
+                    h_banks[c_p, k] = first_product(c_p, k)
+            if live(c_t):
+                for pair in range(2):
+                    x_banks[pair] = transpose_x(c_t, pair)
                 for pair in range(2):
                     regroup_x(c_t, pair, x_banks[pair])
             if live(s + LOAD_AHEAD):
                 load_chunk(s + LOAD_AHEAD)
-            if (s + LOAD_AHEAD - 1) % CHUNKS_PER_ITEM == 0 and live(s + LOAD_AHEAD - 1):
-                load_keys((s + LOAD_AHEAD - 1) // CHUNKS_PER_ITEM)
-
-            if live(c_h):
-                for k in range(PACK):
-                    sum_h(c_h, k, h_banks[k])
-            if live(c_g) and c_g % CHUNKS_PER_ITEM == 0:
-                regroup_keys(c_g // CHUNKS_PER_ITEM)
+            c_keys = s + KEYS_AHEAD
+            if live(c_keys) and c_keys % CHUNKS_PER_ITEM == 0 and c_keys > CHUNKS_PER_ITEM:
+                load_keys(c_keys // CHUNKS_PER_ITEM)
 
             if live(s):
+                quantise_h(s)
+                if s % CHUNKS_PER_ITEM == 0:
+                    quantise_keys(s // CHUNKS_PER_ITEM)
+            if live(c_h):
+                scale_h(c_h)
+            if live(s):
                 for j in range(BLOCKS):
-                    second_product(s, j)
-                    if j % 2 == 1:
-                        store_blocks(s, j - 1)
+                    if s < CHUNKS - 2:
+                        second_product(s, j, nc.scalar.copy)
+                        if j % 2 == 1:
+                            store_blocks(s, j - 1, 2)
+                    elif s == CHUNKS - 2 and j < BLOCKS - 1:
+                        second_product(s, j, nc.scalar.copy)
+                        store_blocks(s, j, 1)
+                    elif s == CHUNKS - 1:
+                        if j == 0:
+                            second_product(s - 1, BLOCKS - 1, nc.vector.tensor_copy)
+                            store_blocks(s - 1, BLOCKS - 1, 1)
+                        second_product(s, j, nc.vector.tensor_copy if j % 2 else nc.scalar.copy)
+                        store_blocks(s, j, 1)
+            if live(c_xq) and c_xq != 1:
+                quantise_x(c_xq)
+            if c_xq == 0:
+                regroup_keys(0, None)
 
         v_sb = keep.tile([P, PACK * C], BF16)
-        nc.sync.dma_start(
-            out=v_sb[:].rearrange("m (half f) -> m half f", half=2),
-            in_=in_proj_v.rearrange("(half m par) c -> m half (par c)", half=2, par=2),
-        )
+        for half in range(2):
+            nc.sync.dma_start(
+                out=v_sb[:, half * 2 * C : (half + 1) * 2 * C],
+                in_=in_proj_v.rearrange("(half m par) c -> half m (par c)", half=2, par=2)[half],
+            )
         g_sb = keep.tile([P, PACK], BF16)
         b_sb = keep.tile([P, PACK], BF16)
         with nc.allow_non_contiguous_dma(reason="gain and bias: two pairs of elements a partition"):
@@ -293,6 +349,8 @@ def tile_attentionlayer_pa_t_kernel(
         load_keys(0)
         for c in range(1, IN_BUFS):
             load_chunk(c)
+            if c == 3:
+                load_keys(1)
 
         ident_f32 = keep.tile([P, P], F32)
         make_identity(nc, ident_f32[:])
@@ -300,28 +358,44 @@ def tile_attentionlayer_pa_t_kernel(
         make_identity(nc, ident_bf16[:])
 
         bias = keep.tile([P, PACK], F32)
-        nc.vector.tensor_copy(out=bias[:], in_=b_sb[:])
         one = keep.tile([P, 1], F32)
         nc.vector.memset(one[:], 1.0)
         nc.scalar.sqrt(out=one[:], in_=one[:])
         squares = keep.tile([P, PACK * C], BF16)
-        sum_squares = keep.tile([P, PACK], F32)
+        pair_cols = [slice(2 * a, 2 * a + 2) for a in range(2)]
+        sum_squares = [keep.tile([P, 2], F32, name="sum_squares%d" % a) for a in range(2)]
+        norm = [keep.tile([P, 2], F32, name="norm%d" % a) for a in range(2)]
+        inv_norm = [keep.tile([P, 2], F32, name="inv_norm%d" % a) for a in range(2)]
+        gain = [keep.tile([P, 2], F32, name="gain%d" % a) for a in range(2)]
         for k in range(PACK):
-            nc.scalar.activation(
-                out=squares[:, k * C : (k + 1) * C],
-                in_=v_sb[:, k * C : (k + 1) * C],
-                func=ACT.Square,
-                accum_out=sum_squares[:, k : k + 1],
-            )
-        norm = keep.tile([P, PACK], F32)
-        nc.scalar.sqrt(out=norm[:], in_=sum_squares[:])
+            group = slice(k * C, (k + 1) * C)
+            total = sum_squares[k // 2][:, k % 2 : k % 2 + 1]
+            if k < 2:
+                nc.scalar.activation(
+                    out=squares[:, group], in_=v_sb[:, group], func=ACT.Square, accum_out=total
+                )
+            else:
+                nc.vector.scalar_tensor_tensor(
+                    out=squares[:, group],
+                    in0=v_sb[:, group],
+                    scalar=1.0,
+                    in1=v_sb[:, group],
+                    op0=ALU.mult,
+                    op1=ALU.mult,
+                    accum_out=total,
+                )
+        nc.vector.tensor_copy(out=bias[:], in_=b_sb[:])
+        for a in range(2):
+            nc.scalar.sqrt(out=norm[a][:], in_=sum_squares[a][:])
 
         pipeline_step(-T_AHEAD)
 
-        inv_norm = keep.tile([P, PACK], F32)
-        nc.vector.reciprocal(out=inv_norm[:], in_=norm[:])
-        gain = keep.tile([P, PACK], F32)
-        nc.vector.tensor_tensor(out=gain[:], in0=inv_norm[:], in1=g_sb[:], op=ALU.mult)
+        for a in range(2):
+            nc.vector.reciprocal(out=inv_norm[a][:], in_=norm[a][:])
+        for a in range(2):
+            nc.vector.tensor_tensor(
+                out=gain[a][:], in0=inv_norm[a][:], in1=g_sb[:, pair_cols[a]], op=ALU.mult
+            )
 
         w_sorted = keep.tile([P, PACK * C], BF16)
         for k in range(PACK):
@@ -332,29 +406,34 @@ def tile_attentionlayer_pa_t_kernel(
                 in0=v_sb[:, k * C : (k + 1) * C].rearrange(
                     "m (half q par) -> m half par q", half=2, par=2
                 ),
-                scalar1=gain[:, k : k + 1],
+                scalar1=gain[k // 2][:, k % 2 : k % 2 + 1],
             )
         w_grouped = keep.tile([P, PACK * P * PACK], BF16, align_bytes=64)
+        w_codes = keep.tile([P, PACK * P], U32, align_bytes=64)
+        w_scales = keep.tile([P, PACK * P], U8, align_bytes=64)
         for a in range(2):
-            bank = psum.tile([P, 2 * PACK * P], BF16, name="wT", tag="bank")
+            pool, tag = (psum, "bank") if a == 0 else (psum_h, "bank_h")
+            bank = pool.tile([P, 2 * PACK * P], BF16, name="wT", tag=tag)
             for i in range(2 * PACK):
                 nc.tensor.transpose(
                     bank[:, i * P : (i + 1) * P],
                     w_sorted[:, (a * 2 * PACK + i) * P : (a * 2 * PACK + i + 1) * P],
                     ident_bf16[:],
                 )
-            copy_out = nc.vector.tensor_copy if a == 0 else nc.scalar.copy
+            copy_out = nc.scalar.copy if a == 0 else nc.vector.tensor_copy
             copy_out(
                 out=w_grouped[:, a * 2 * C : (a + 1) * 2 * C].rearrange(
                     "q (g m k) -> q g m k", g=2, k=PACK
                 ),
                 in_=bank[:].rearrange("q (g k m) -> q g m k", g=2, k=PACK),
             )
-        w_codes = keep.tile([P, PACK * P], U32, align_bytes=64)
-        w_scales = keep.tile([P, PACK * P], U8, align_bytes=64)
-        nc.vector.quantize_mx(
-            out=w_codes[:].bitcast(FP8X4), scales=w_scales[:], in_=w_grouped[:]
-        )
+        for a in range(2):
+            words = slice(a * 2 * P, (a + 1) * 2 * P)
+            nc.vector.quantize_mx(
+                out=w_codes[:, words].bitcast(FP8X4),
+                scales=w_scales[:, words],
+                in_=w_grouped[:, a * 2 * C : (a + 1) * 2 * C],
+            )
 
         for s in range(1 - T_AHEAD, CHUNKS):
             pipeline_step(s)

@@ -25,7 +25,7 @@ T_AHEAD = 4
 XQ_AHEAD = 3
 P_AHEAD = 2
 H_AHEAD = 1
-G_BLOCKS = 1
+RUN = 4
 LOAD_AHEAD = 10
 KEYS_AHEAD = 8
 KEY_PARTS = 4
@@ -190,47 +190,41 @@ def tile_attentionlayer_pa_t_kernel(
 
         def sum_h(c, k, bank):
             if k == 0:
-                h_sum[c] = two.tile([P, PACK, CHUNK], F32, name="h_sum", tag="h_sum")
+                h_sum[c] = two.tile(
+                    [P, CHUNK // RUN, PACK, RUN], F32, name="h_sum", tag="h_sum", align_bytes=64
+                )
             pairs = te_T[c][:].bitcast(BF16).rearrange(
                 "q (half r par) -> q half r par", half=2, par=2
             )
             nc.vector.scalar_tensor_tensor(
-                out=h_sum[c][:, k, :],
-                in0=bank[:],
+                out=h_sum[c][:, :, k, :],
+                in0=bank[:].rearrange("q (b i) -> q b i", i=RUN),
                 scalar=bias[:, k : k + 1],
-                in1=pairs[:, k // 2, :, k % 2],
+                in1=pairs[:, k // 2, :, k % 2].rearrange("q (b i) -> q b i", i=RUN),
                 op0=ALU.add,
                 op1=ALU.add,
             )
 
-        def shared_with_scalar(c):
-            return not live(c - H_AHEAD + T_AHEAD)
-
-        def scaled(c, first, last):
-            runs = slice(first * P // 4, last * P // 4)
-            return (
-                h_grouped[c][:].rearrange("q (b i k) -> q b k i", i=4, k=PACK)[:, runs],
-                h_sum[c][:].rearrange("q k (b i) -> q b k i", i=4)[:, runs],
-            )
+        def scalar_blocks(c):
+            return 0 if live(c - H_AHEAD + T_AHEAD) else BLOCKS // 2
 
         def scale_h(c):
             h_grouped[c] = two.tile(
                 [P, CHUNK * PACK], BF16, name="h_grouped", tag="h_grouped", align_bytes=64
             )
-            blocks = BLOCKS // 2 if shared_with_scalar(c) else BLOCKS - G_BLOCKS
-            h_out, h_in = scaled(c, 0, blocks)
+            h_out = h_grouped[c][:].rearrange("q (b i k) -> q b k i", i=RUN, k=PACK)
+            cut = (BLOCKS - scalar_blocks(c)) * P // RUN
             nc.vector.tensor_scalar(
-                out=h_out, in0=h_in, scalar1=SQRT_HALF, scalar2=None, op0=ALU.mult
+                out=h_out[:, :cut],
+                in0=h_sum[c][:, :cut],
+                scalar1=SQRT_HALF,
+                scalar2=None,
+                op0=ALU.mult,
             )
-            if shared_with_scalar(c):
-                h_out, h_in = scaled(c, blocks, BLOCKS)
-                nc.scalar.activation(out=h_out, in_=h_in, func=ACT.Copy, scale=SQRT_HALF)
-
-        def scale_h_gpsimd(c):
-            h_out, h_in = scaled(c, BLOCKS - G_BLOCKS, BLOCKS)
-            nc.gpsimd.tensor_scalar(
-                out=h_out, in0=h_in, scalar1=SQRT_HALF, scalar2=0.0, op0=ALU.mult, op1=ALU.add
-            )
+            if scalar_blocks(c):
+                nc.scalar.activation(
+                    out=h_out[:, cut:], in_=h_sum[c][:, cut:], func=ACT.Copy, scale=SQRT_HALF
+                )
 
         def quantise_h(c):
             h_codes[c] = two.tile([P, CHUNK], U32, name="h_codes", tag="h_codes", align_bytes=64)
@@ -265,37 +259,54 @@ def tile_attentionlayer_pa_t_kernel(
 
         h_banks = {}
 
+        def transposes(c):
+            if live(c):
+                for half in range(2):
+                    copy_te(c, half, transpose_te(c, half))
+
+        def transposes_x(c):
+            if live(c):
+                for pair in range(2):
+                    regroup_x(c, pair, transpose_x(c, pair))
+
+        def products(c):
+            if live(c):
+                for k in range(PACK):
+                    h_banks[c, k] = first_product(c, k)
+
+        def scores(c):
+            last = c == CHUNKS - 1
+            for j in range(BLOCKS):
+                second_product(c, j, nc.vector.tensor_copy if last and j % 2 else nc.scalar.copy)
+                if c >= CHUNKS - 2:
+                    store_blocks(c, j, 1)
+                elif j % 2 == 1:
+                    store_blocks(c, j - 1, 2)
+
         def pipeline_step(s):
             c_t, c_xq, c_p, c_h = s + T_AHEAD, s + XQ_AHEAD, s + P_AHEAD, s + H_AHEAD
-            x_banks, te_banks = {}, {}
+            early = s == CHUNKS - 2
 
+            if early:
+                quantise_h(s)
+                scores(s)
             if live(c_h):
                 for k in range(PACK):
                     sum_h(c_h, k, h_banks[c_h, k])
             if c_h == 0:
                 quantise_x(1)
-            if live(s):
-                if live(c_xq - 1):
-                    hold_gpsimd(x_codes[c_xq - 1])
-                if not shared_with_scalar(s):
-                    scale_h_gpsimd(s)
-                n, part = divmod(s, CHUNKS_PER_ITEM)
-                if n + 1 < BATCH:
-                    regroup_keys(n + 1, part)
+            n, part = divmod(s, CHUNKS_PER_ITEM)
+            if live(s) and n + 1 < BATCH:
+                hold_gpsimd(x_codes[c_xq - 1])
+                regroup_keys(n + 1, part)
 
-            if live(c_t):
-                for half in range(2):
-                    te_banks[half] = transpose_te(c_t, half)
-                for half in range(2):
-                    copy_te(c_t, half, te_banks[half])
-            if live(c_p):
-                for k in range(PACK):
-                    h_banks[c_p, k] = first_product(c_p, k)
-            if live(c_t):
-                for pair in range(2):
-                    x_banks[pair] = transpose_x(c_t, pair)
-                for pair in range(2):
-                    regroup_x(c_t, pair, x_banks[pair])
+            if s < 0:
+                products(c_p)
+                transposes(c_t)
+            else:
+                transposes(c_t)
+                products(c_p)
+            transposes_x(c_t)
             if live(s + LOAD_AHEAD):
                 load_chunk(s + LOAD_AHEAD)
             c_keys = s + KEYS_AHEAD
@@ -303,26 +314,14 @@ def tile_attentionlayer_pa_t_kernel(
                 load_keys(c_keys // CHUNKS_PER_ITEM)
 
             if live(s):
-                quantise_h(s)
+                if not early:
+                    quantise_h(s)
                 if s % CHUNKS_PER_ITEM == 0:
                     quantise_keys(s // CHUNKS_PER_ITEM)
             if live(c_h):
                 scale_h(c_h)
-            if live(s):
-                for j in range(BLOCKS):
-                    if s < CHUNKS - 2:
-                        second_product(s, j, nc.scalar.copy)
-                        if j % 2 == 1:
-                            store_blocks(s, j - 1, 2)
-                    elif s == CHUNKS - 2 and j < BLOCKS - 1:
-                        second_product(s, j, nc.scalar.copy)
-                        store_blocks(s, j, 1)
-                    elif s == CHUNKS - 1:
-                        if j == 0:
-                            second_product(s - 1, BLOCKS - 1, nc.vector.tensor_copy)
-                            store_blocks(s - 1, BLOCKS - 1, 1)
-                        second_product(s, j, nc.vector.tensor_copy if j % 2 else nc.scalar.copy)
-                        store_blocks(s, j, 1)
+            if live(s) and not early:
+                scores(s)
             if live(c_xq) and c_xq != 1:
                 quantise_x(c_xq)
             if c_xq == 0:

@@ -206,7 +206,22 @@ def tile_attentionlayer_pa_t_kernel(
             )
 
         def scalar_blocks(c):
-            return 0 if live(c - H_AHEAD + T_AHEAD) else BLOCKS // 2
+            return 2 if c in (13, 14) else 0
+
+        def gps(c):
+            return 1 if c < 13 else 0
+
+        def scale_g(c):
+            h_out = h_grouped[c][:].rearrange("q (b i k) -> q b k i", i=RUN, k=PACK)
+            cut = (BLOCKS - gps(c)) * P // RUN
+            nc.gpsimd.tensor_scalar(
+                out=h_out[:, cut:],
+                in0=h_sum[c][:, cut:],
+                scalar1=SQRT_HALF,
+                scalar2=0.0,
+                op0=ALU.mult,
+                op1=ALU.add,
+            )
 
         def scale_h(c):
             h_grouped[c] = two.tile(
@@ -214,6 +229,19 @@ def tile_attentionlayer_pa_t_kernel(
             )
             h_out = h_grouped[c][:].rearrange("q (b i k) -> q b k i", i=RUN, k=PACK)
             cut = (BLOCKS - scalar_blocks(c)) * P // RUN
+            if c == CHUNKS - 1:
+                for part in range(2):
+                    runs = slice(part * CHUNK // RUN // 2, (part + 1) * CHUNK // RUN // 2)
+                    nc.vector.tensor_scalar(
+                        out=h_out[:, runs],
+                        in0=h_sum[c][:, runs],
+                        scalar1=SQRT_HALF,
+                        scalar2=None,
+                        op0=ALU.mult,
+                    )
+                return
+            if gps(c):
+                cut = (BLOCKS - gps(c)) * P // RUN
             nc.vector.tensor_scalar(
                 out=h_out[:, :cut],
                 in0=h_sum[c][:, :cut],
@@ -259,6 +287,13 @@ def tile_attentionlayer_pa_t_kernel(
 
         h_banks = {}
 
+        def warm(count):
+            bank = psum_h.tile([P, CHUNK], F32, name="warm", tag="bank_h")
+            for i in range(count):
+                nc.tensor.matmul(
+                    out=bank[:], lhsT=zeros[:, 0:P], rhs=zeros[:], start=True, stop=True
+                )
+
         def transposes(c):
             if live(c):
                 for half in range(2):
@@ -269,9 +304,9 @@ def tile_attentionlayer_pa_t_kernel(
                 for pair in range(2):
                     regroup_x(c, pair, transpose_x(c, pair))
 
-        def products(c):
+        def products(c, codes):
             if live(c):
-                for k in range(PACK):
+                for k in codes:
                     h_banks[c, k] = first_product(c, k)
 
         def scores(c):
@@ -296,17 +331,23 @@ def tile_attentionlayer_pa_t_kernel(
             if c_h == 0:
                 quantise_x(1)
             n, part = divmod(s, CHUNKS_PER_ITEM)
-            if live(s) and n + 1 < BATCH:
-                hold_gpsimd(x_codes[c_xq - 1])
-                regroup_keys(n + 1, part)
+            if live(s) and (gps(s) or n + 1 < BATCH):
+                if live(c_xq - 1):
+                    hold_gpsimd(x_codes[c_xq - 1])
+                if gps(s):
+                    scale_g(s)
+                if n + 1 < BATCH and True:
+                    regroup_keys(n + 1, part)
 
             if s < 0:
-                products(c_p)
+                products(c_p, range(PACK))
                 transposes(c_t)
             else:
                 transposes(c_t)
-                products(c_p)
+                products(c_p, range(2))
             transposes_x(c_t)
+            if s >= 0:
+                products(c_p, range(2, PACK))
             if live(s + LOAD_AHEAD):
                 load_chunk(s + LOAD_AHEAD)
             c_keys = s + KEYS_AHEAD
@@ -359,6 +400,9 @@ def tile_attentionlayer_pa_t_kernel(
         bias = keep.tile([P, PACK], F32)
         one = keep.tile([P, 1], F32)
         nc.vector.memset(one[:], 1.0)
+        zeros = keep.tile([P, CHUNK], BF16)
+        nc.vector.memset(zeros[:], 0.0)
+        warm(8)
         nc.scalar.sqrt(out=one[:], in_=one[:])
         squares = keep.tile([P, PACK * C], BF16)
         pair_cols = [slice(2 * a, 2 * a + 2) for a in range(2)]
@@ -388,6 +432,7 @@ def tile_attentionlayer_pa_t_kernel(
             nc.scalar.sqrt(out=norm[a][:], in_=sum_squares[a][:])
 
         pipeline_step(-T_AHEAD)
+        warm(2)
 
         for a in range(2):
             nc.vector.reciprocal(out=inv_norm[a][:], in_=norm[a][:])
@@ -434,5 +479,6 @@ def tile_attentionlayer_pa_t_kernel(
                 in_=w_grouped[:, a * 2 * C : (a + 1) * 2 * C],
             )
 
+        warm(2)
         for s in range(1 - T_AHEAD, CHUNKS):
             pipeline_step(s)

@@ -66,13 +66,13 @@ def tile_attentionlayer_pa_t_kernel(
 
         def load_chunk(c):
             rows = slice(c * CHUNK, (c + 1) * CHUNK)
-            te_in[c] = te_pool.tile([P, BLOCKS * E], BF16, name="te_in", tag="te_in")
-            nc.sync.dma_start(
-                out=te_in[c][:], in_=te_rows[rows, :].rearrange("(p j) e -> p (j e)", j=BLOCKS)
-            )
             x_in[c] = x_pool.tile([P, BLOCKS * C], BF16, name="x_in", tag="x_in")
             nc.sync.dma_start(
                 out=x_in[c][:], in_=x_rows[rows, :].rearrange("(p j) c -> p (j c)", j=BLOCKS)
+            )
+            te_in[c] = te_pool.tile([P, BLOCKS * E], BF16, name="te_in", tag="te_in")
+            nc.sync.dma_start(
+                out=te_in[c][:], in_=te_rows[rows, :].rearrange("(p j) e -> p (j e)", j=BLOCKS)
             )
 
         def load_keys(n):
@@ -241,7 +241,7 @@ def tile_attentionlayer_pa_t_kernel(
                     )
                 return
             if gps(c):
-                cut = (BLOCKS - gps(c)) * P // RUN
+                cut = (BLOCKS - gps(c)) * P // RUN + 2
             nc.vector.tensor_scalar(
                 out=h_out[:, :cut],
                 in0=h_sum[c][:, :cut],
@@ -332,21 +332,19 @@ def tile_attentionlayer_pa_t_kernel(
                 quantise_x(1)
             n, part = divmod(s, CHUNKS_PER_ITEM)
             if live(s) and (gps(s) or n + 1 < BATCH):
-                if live(c_xq - 1):
-                    hold_gpsimd(x_codes[c_xq - 1])
                 if gps(s):
                     scale_g(s)
                 if n + 1 < BATCH and True:
                     regroup_keys(n + 1, part)
 
-            if s < 0:
+            if s < -1:
                 products(c_p, range(PACK))
-                transposes(c_t)
+                transposes_x(c_t)
             else:
-                transposes(c_t)
+                transposes_x(c_t)
                 products(c_p, range(2))
-            transposes_x(c_t)
-            if s >= 0:
+            transposes(c_t)
+            if s >= -1:
                 products(c_p, range(2, PACK))
             if live(s + LOAD_AHEAD):
                 load_chunk(s + LOAD_AHEAD)
@@ -357,16 +355,14 @@ def tile_attentionlayer_pa_t_kernel(
             if live(s):
                 if not early:
                     quantise_h(s)
-                if s % CHUNKS_PER_ITEM == 0:
+                if s % CHUNKS_PER_ITEM == 0 and s > 0:
                     quantise_keys(s // CHUNKS_PER_ITEM)
+            if c_xq > 1 and live(c_xq):
+                quantise_x(c_xq)
             if live(c_h):
                 scale_h(c_h)
             if live(s) and not early:
                 scores(s)
-            if live(c_xq) and c_xq != 1:
-                quantise_x(c_xq)
-            if c_xq == 0:
-                regroup_keys(0, None)
 
         v_sb = keep.tile([P, PACK * C], BF16)
         for half in range(2):
@@ -394,8 +390,6 @@ def tile_attentionlayer_pa_t_kernel(
 
         ident_f32 = keep.tile([P, P], F32)
         make_identity(nc, ident_f32[:])
-        ident_bf16 = keep.tile([P, P], BF16)
-        make_identity(nc, ident_bf16[:])
 
         bias = keep.tile([P, PACK], F32)
         one = keep.tile([P, 1], F32)
@@ -441,35 +435,33 @@ def tile_attentionlayer_pa_t_kernel(
                 out=gain[a][:], in0=inv_norm[a][:], in1=g_sb[:, pair_cols[a]], op=ALU.mult
             )
 
-        w_sorted = keep.tile([P, PACK * C], BF16)
+        w_rows = keep.tile([P, PACK * C], BF16)
         for k in range(PACK):
             nc.vector.tensor_scalar_mul(
-                out=w_sorted[:, k * C : (k + 1) * C].rearrange(
-                    "m (half par q) -> m half par q", half=2, par=2
-                ),
-                in0=v_sb[:, k * C : (k + 1) * C].rearrange(
-                    "m (half q par) -> m half par q", half=2, par=2
-                ),
+                out=w_rows[:, k * C : (k + 1) * C],
+                in0=v_sb[:, k * C : (k + 1) * C],
                 scalar1=gain[k // 2][:, k % 2 : k % 2 + 1],
             )
+        w_words = w_rows[:].bitcast(F32)
+        quantise_x(0)
+        regroup_keys(0, None)
         w_grouped = keep.tile([P, PACK * P * PACK], BF16, align_bytes=64)
         w_codes = keep.tile([P, PACK * P], U32, align_bytes=64)
         w_scales = keep.tile([P, PACK * P], U8, align_bytes=64)
         for a in range(2):
             pool, tag = (psum, "bank") if a == 0 else (psum_h, "bank_h")
-            bank = pool.tile([P, 2 * PACK * P], BF16, name="wT", tag=tag)
-            for i in range(2 * PACK):
+            bank = pool.tile([P, PACK * P], F32, name="wT", tag=tag)
+            for i in range(PACK):
+                word0 = (a * PACK + i) * P
                 nc.tensor.transpose(
-                    bank[:, i * P : (i + 1) * P],
-                    w_sorted[:, (a * 2 * PACK + i) * P : (a * 2 * PACK + i + 1) * P],
-                    ident_bf16[:],
+                    bank[:, i * P : (i + 1) * P], w_words[:, word0 : word0 + P], ident_f32[:]
                 )
             copy_out = nc.scalar.copy if a == 0 else nc.vector.tensor_copy
             copy_out(
-                out=w_grouped[:, a * 2 * C : (a + 1) * 2 * C].rearrange(
-                    "q (g m k) -> q g m k", g=2, k=PACK
-                ),
-                in_=bank[:].rearrange("q (g k m) -> q g m k", g=2, k=PACK),
+                out=w_grouped[:]
+                .bitcast(F32)[:, a * C : (a + 1) * C]
+                .rearrange("q (g m half) -> q g m half", g=2, half=2),
+                in_=bank[:].rearrange("q (g half m) -> q g m half", g=2, half=2),
             )
         for a in range(2):
             words = slice(a * 2 * P, (a + 1) * 2 * P)
@@ -478,6 +470,7 @@ def tile_attentionlayer_pa_t_kernel(
                 scales=w_scales[:, words],
                 in_=w_grouped[:, a * 2 * C : (a + 1) * 2 * C],
             )
+        quantise_keys(0)
 
         warm(2)
         for s in range(1 - T_AHEAD, CHUNKS):

@@ -188,19 +188,20 @@ def tile_attentionlayer_pa_t_kernel(
             )
             return bank
 
-        def sum_h(c, k, bank):
-            if k == 0:
+        def sum_h(c, k, bank, first=0, last=BLOCKS):
+            if k == 0 and first == 0:
                 h_sum[c] = two.tile(
                     [P, CHUNK // RUN, PACK, RUN], F32, name="h_sum", tag="h_sum", align_bytes=64
                 )
             pairs = te_T[c][:].bitcast(BF16).rearrange(
                 "q (half r par) -> q half r par", half=2, par=2
             )
+            runs = slice(first * P // RUN, last * P // RUN)
             nc.vector.scalar_tensor_tensor(
-                out=h_sum[c][:, :, k, :],
-                in0=bank[:].rearrange("q (b i) -> q b i", i=RUN),
+                out=h_sum[c][:, runs, k, :],
+                in0=bank[:].rearrange("q (b i) -> q b i", i=RUN)[:, runs],
                 scalar=bias[:, k : k + 1],
-                in1=pairs[:, k // 2, :, k % 2].rearrange("q (b i) -> q b i", i=RUN),
+                in1=pairs[:, k // 2, :, k % 2].rearrange("q (b i) -> q b i", i=RUN)[:, runs],
                 op0=ALU.add,
                 op1=ALU.add,
             )
@@ -229,17 +230,6 @@ def tile_attentionlayer_pa_t_kernel(
             )
             h_out = h_grouped[c][:].rearrange("q (b i k) -> q b k i", i=RUN, k=PACK)
             cut = (BLOCKS - scalar_blocks(c)) * P // RUN
-            if c == CHUNKS - 1:
-                for part in range(2):
-                    runs = slice(part * CHUNK // RUN // 2, (part + 1) * CHUNK // RUN // 2)
-                    nc.vector.tensor_scalar(
-                        out=h_out[:, runs],
-                        in0=h_sum[c][:, runs],
-                        scalar1=SQRT_HALF,
-                        scalar2=None,
-                        op0=ALU.mult,
-                    )
-                return
             if gps(c):
                 cut = (BLOCKS - gps(c)) * P // RUN + 2
             nc.vector.tensor_scalar(
@@ -254,18 +244,17 @@ def tile_attentionlayer_pa_t_kernel(
                     out=h_out[:, cut:], in_=h_sum[c][:, cut:], func=ACT.Copy, scale=SQRT_HALF
                 )
 
-        def quantise_h(c):
-            h_codes[c] = two.tile([P, CHUNK], U32, name="h_codes", tag="h_codes", align_bytes=64)
-            h_scales[c] = two.tile([P, CHUNK], U8, name="h_scales", tag="h_scales", align_bytes=64)
-            parts = 2 if c == CHUNKS - 1 else 1
-            for part in range(parts):
-                words = slice(part * CHUNK // parts, (part + 1) * CHUNK // parts)
-                values = slice(part * CHUNK // parts * PACK, (part + 1) * CHUNK // parts * PACK)
-                nc.vector.quantize_mx(
-                    out=h_codes[c][:, words].bitcast(FP8X4),
-                    scales=h_scales[c][:, words],
-                    in_=h_grouped[c][:, values],
-                )
+        def quantise_h(c, part=0, parts=1):
+            if part == 0:
+                h_codes[c] = two.tile([P, CHUNK], U32, name="h_codes", tag="h_codes", align_bytes=64)
+                h_scales[c] = two.tile([P, CHUNK], U8, name="h_scales", tag="h_scales", align_bytes=64)
+            words = slice(part * CHUNK // parts, (part + 1) * CHUNK // parts)
+            values = slice(part * CHUNK // parts * PACK, (part + 1) * CHUNK // parts * PACK)
+            nc.vector.quantize_mx(
+                out=h_codes[c][:, words].bitcast(FP8X4),
+                scales=h_scales[c][:, words],
+                in_=h_grouped[c][:, values],
+            )
 
         def second_product(c, j, copy_out):
             block = slice(j * P, (j + 1) * P)
@@ -318,6 +307,34 @@ def tile_attentionlayer_pa_t_kernel(
                 elif j % 2 == 1:
                     store_blocks(c, j - 1, 2)
 
+        def last_h(c):
+            half = BLOCKS // 2
+            h_grouped[c] = two.tile(
+                [P, CHUNK * PACK], BF16, name="h_grouped", tag="h_grouped", align_bytes=64
+            )
+
+            def scale_half(i):
+                runs = slice(i * half * P // RUN, (i + 1) * half * P // RUN)
+                h_out = h_grouped[c][:].rearrange("q (b i k) -> q b k i", i=RUN, k=PACK)
+                nc.vector.tensor_scalar(
+                    out=h_out[:, runs],
+                    in0=h_sum[c][:, runs],
+                    scalar1=SQRT_HALF,
+                    scalar2=None,
+                    op0=ALU.mult,
+                )
+
+            for k in range(PACK):
+                sum_h(c, k, h_banks[c, k], 0, half)
+            for k in range(2):
+                sum_h(c, k, h_banks[c, k], half, BLOCKS)
+            scale_half(0)
+            for k in range(2, PACK):
+                sum_h(c, k, h_banks[c, k], half, BLOCKS)
+            quantise_h(c, 0, 2)
+            scale_half(1)
+            quantise_h(c, 1, 2)
+
         def pipeline_step(s):
             c_t, c_xq, c_p, c_h = s + T_AHEAD, s + XQ_AHEAD, s + P_AHEAD, s + H_AHEAD
             early = s == CHUNKS - 2
@@ -325,7 +342,9 @@ def tile_attentionlayer_pa_t_kernel(
             if early:
                 quantise_h(s)
                 scores(s)
-            if live(c_h):
+            if early:
+                last_h(c_h)
+            elif live(c_h):
                 for k in range(PACK):
                     sum_h(c_h, k, h_banks[c_h, k])
             if c_h == 0:
@@ -342,9 +361,9 @@ def tile_attentionlayer_pa_t_kernel(
                 transposes_x(c_t)
             else:
                 transposes_x(c_t)
-                products(c_p, range(2))
+                products(c_p, range(2 if s >= 0 else PACK))
             transposes(c_t)
-            if s >= -1:
+            if s >= 0:
                 products(c_p, range(2, PACK))
             if live(s + LOAD_AHEAD):
                 load_chunk(s + LOAD_AHEAD)
@@ -353,13 +372,13 @@ def tile_attentionlayer_pa_t_kernel(
                 load_keys(c_keys // CHUNKS_PER_ITEM)
 
             if live(s):
-                if not early:
+                if not early and s < CHUNKS - 1:
                     quantise_h(s)
                 if s % CHUNKS_PER_ITEM == 0 and s > 0:
                     quantise_keys(s // CHUNKS_PER_ITEM)
             if c_xq > 1 and live(c_xq):
                 quantise_x(c_xq)
-            if live(c_h):
+            if live(c_h) and not early:
                 scale_h(c_h)
             if live(s) and not early:
                 scores(s)

from contextlib import ExitStack
import math

import concourse.mybir as mybir
from concourse.masks import make_identity

F32 = mybir.dt.float32
BF16 = mybir.dt.bfloat16
U32 = mybir.dt.uint32
U8 = mybir.dt.uint8
FP8X4 = mybir.dt.float8_e4m3fn_x4
ACT = mybir.ActivationFunctionType
ALU = mybir.AluOpType

P = 128
PACK = 4
BATCH, TQ, TS, C, E = 4, 2048, 512, 512, 512
BLOCKS = 4
CHUNK = BLOCKS * P
CHUNKS = BATCH * TQ // CHUNK
CHUNKS_PER_ITEM = TQ // CHUNK
SQRT_HALF = math.sqrt(0.5)

T_AHEAD = 4
XQ_AHEAD = 3
P_AHEAD = 2
H_AHEAD = 1
RUN = 4
LOAD_AHEAD = 10
KEYS_AHEAD = 8
KEY_PARTS = 4
IN_BUFS = LOAD_AHEAD - T_AHEAD

FLOPS = 2 * BATCH * TQ * C * E + 2 * BATCH * TQ * E * TS


def tile_attentionlayer_pa_t_kernel(
    tc, x, target_embedding, encoder_keys, in_proj_v, in_proj_g, in_proj_b, out
):
    nc = tc.nc
    x_rows = x.flatten_outer_dims()
    te_rows = target_embedding.flatten_outer_dims()
    out_rows = out.flatten_outer_dims()

    with ExitStack() as ctx:
        ctx.enter_context(tc.manual_schedule())

        keep = ctx.enter_context(tc.tile_pool(name="keep", bufs=1))
        x_pool = ctx.enter_context(tc.tile_pool(name="x_pool", bufs=IN_BUFS))
        te_pool = ctx.enter_context(tc.tile_pool(name="te_pool", bufs=IN_BUFS))
        key_pool = ctx.enter_context(tc.tile_pool(name="key_pool", bufs=2))
        two = ctx.enter_context(tc.tile_pool(name="two", bufs=2))
        three = ctx.enter_context(tc.tile_pool(name="three", bufs=3))
        four = ctx.enter_context(tc.tile_pool(name="four", bufs=4))
        psum = ctx.enter_context(tc.psum_pool(name="psum", bufs=4))
        psum_h = ctx.enter_context(tc.psum_pool(name="psum_h", bufs=4))

        x_in, te_in, key_in = {}, {}, {}
        x_grouped, x_codes, x_scales = {}, {}, {}
        te_T = {}
        h_sum, h_grouped, h_codes, h_scales = {}, {}, {}, {}
        out_sb = {}

        def live(c):
            return 0 <= c < CHUNKS

        def load_chunk(c):
            rows = slice(c * CHUNK, (c + 1) * CHUNK)
            x_in[c] = x_pool.tile([P, BLOCKS * C], BF16, name="x_in", tag="x_in")
            nc.sync.dma_start(
                out=x_in[c][:], in_=x_rows[rows, :].rearrange("(p j) c -> p (j c)", j=BLOCKS)
            )
            te_in[c] = te_pool.tile([P, BLOCKS * E], BF16, name="te_in", tag="te_in")
            nc.sync.dma_start(
                out=te_in[c][:], in_=te_rows[rows, :].rearrange("(p j) e -> p (j e)", j=BLOCKS)
            )

        def load_keys(n):
            key_in[n] = key_pool.tile([P, PACK * TS], BF16, name="key_in", tag="key_in")
            nc.sync.dma_start(
                out=key_in[n][:].rearrange("q (half f) -> q half f", half=2),
                in_=encoder_keys[n].rearrange("(half q par) s -> q half (par s)", half=2, par=2),
            )

        def store_blocks(c, first, count):
            rows = slice(c * CHUNK, (c + 1) * CHUNK)
            cols = slice(first * TS, (first + count) * TS)
            nc.sync.dma_start(
                out=out_rows[rows, :].rearrange("(p j) s -> p (j s)", j=BLOCKS)[:, cols],
                in_=out_sb[c][:, cols],
            )

        key_codes = keep.tile([P, BATCH * TS], U32, align_bytes=64)
        key_scales = keep.tile([P, BATCH * TS], U8, align_bytes=64)
        key_grouped = {}

        def regroup_keys(n, part):
            if not part:
                key_grouped[n] = key_pool.tile(
                    [P, TS * PACK], BF16, name="key_grouped", tag="key_grouped", align_bytes=64
                )
            keys_out = key_grouped[n][:].rearrange("q (b i k) -> q b k i", i=4, k=PACK)
            keys_in = key_in[n][:].rearrange("q (k b i) -> q b k i", k=PACK, i=4)
            if part is None:
                nc.vector.tensor_copy(out=keys_out, in_=keys_in)
            else:
                runs = slice(part * TS // 4 // KEY_PARTS, (part + 1) * TS // 4 // KEY_PARTS)
                nc.gpsimd.tensor_scalar(
                    out=keys_out[:, runs],
                    in0=keys_in[:, runs],
                    scalar1=1.0,
                    scalar2=0.0,
                    op0=ALU.mult,
                    op1=ALU.add,
                )

        def hold_gpsimd(codes):
            seen = two.tile([P, 1], U32, name="seen", tag="seen")
            nc.gpsimd.tensor_copy(out=seen[:], in_=codes[:, 0:1])

        def quantise_keys(n):
            cols = slice(n * TS, (n + 1) * TS)
            nc.vector.quantize_mx(
                out=key_codes[:, cols].bitcast(FP8X4),
                scales=key_scales[:, cols],
                in_=key_grouped[n][:],
            )

        def transpose_x(c, pair):
            x_words = x_in[c][:].bitcast(F32)
            bank = psum.tile([P, 4 * P], F32, name="xT", tag="bank")
            for b in range(2):
                for half in range(2):
                    word0 = (2 * pair + b) * (C // 2) + half * P
                    nc.tensor.transpose(
                        bank[:, (2 * half + b) * P : (2 * half + b + 1) * P],
                        x_words[:, word0 : word0 + P],
                        ident_f32[:],
                    )
            return bank

        def regroup_x(c, pair, bank):
            if pair == 0:
                x_grouped[c] = three.tile(
                    [P, CHUNK * PACK], BF16, name="x_grouped", tag="x_grouped", align_bytes=64
                )
            words = x_grouped[c][:].bitcast(F32)
            nc.scalar.copy(
                out=words[:, pair * 4 * P : (pair + 1) * 4 * P].rearrange(
                    "q (r half) -> q r half", half=2
                ),
                in_=bank[:].rearrange("q (half r) -> q r half", half=2),
            )

        def quantise_x(c):
            x_codes[c] = three.tile([P, CHUNK], U32, name="x_codes", tag="x_codes", align_bytes=64)
            x_scales[c] = three.tile([P, CHUNK], U8, name="x_scales", tag="x_scales", align_bytes=64)
            nc.vector.quantize_mx(
                out=x_codes[c][:].bitcast(FP8X4), scales=x_scales[c][:], in_=x_grouped[c][:]
            )

        def transpose_te(c, half):
            te_words = te_in[c][:].bitcast(F32)
            bank = psum.tile([P, CHUNK], F32, name="teT", tag="bank")
            for j in range(BLOCKS):
                word0 = j * (E // 2) + half * P
                nc.tensor.transpose(
                    bank[:, j * P : (j + 1) * P], te_words[:, word0 : word0 + P], ident_f32[:]
                )
            return bank

        def copy_te(c, half, bank):
            if half == 0:
                te_T[c] = four.tile([P, 2 * CHUNK], F32, name="te_T", tag="te_T")
            nc.scalar.copy(out=te_T[c][:, half * CHUNK : (half + 1) * CHUNK], in_=bank[:])

        def first_product(c, k):
            group = slice(k * P, (k + 1) * P)
            bank = psum_h.tile([P, CHUNK], F32, name="hT", tag="bank_h")
            nc.tensor.matmul_mx(
                out=bank[:],
                lhsT=w_codes[:, group].bitcast(FP8X4),
                lhsT_scale=w_scales[:, group],
                rhs=x_codes[c][:].bitcast(FP8X4),
                rhs_scale=x_scales[c][:],
                start=True,
                stop=True,
            )
            return bank

        def sum_h(c, k, bank, first=0, last=BLOCKS):
            if k == 0 and first == 0:
                h_sum[c] = two.tile(
                    [P, CHUNK // RUN, PACK, RUN], F32, name="h_sum", tag="h_sum", align_bytes=64
                )
            pairs = te_T[c][:].bitcast(BF16).rearrange(
                "q (half r par) -> q half r par", half=2, par=2
            )
            runs = slice(first * P // RUN, last * P // RUN)
            nc.vector.scalar_tensor_tensor(
                out=h_sum[c][:, runs, k, :],
                in0=bank[:].rearrange("q (b i) -> q b i", i=RUN)[:, runs],
                scalar=bias[:, k : k + 1],
                in1=pairs[:, k // 2, :, k % 2].rearrange("q (b i) -> q b i", i=RUN)[:, runs],
                op0=ALU.add,
                op1=ALU.add,
            )

        def scalar_blocks(c):
            return 2 if c in (13, 14) else 0

        def gps(c):
            return 1 if c < 13 else 0

        def scale_g(c):
            h_out = h_grouped[c][:].rearrange("q (b i k) -> q b k i", i=RUN, k=PACK)
            cut = (BLOCKS - gps(c)) * P // RUN
            nc.gpsimd.tensor_scalar(
                out=h_out[:, cut:],
                in0=h_sum[c][:, cut:],
                scalar1=SQRT_HALF,
                scalar2=0.0,
                op0=ALU.mult,
                op1=ALU.add,
            )

        def scale_h(c):
            h_grouped[c] = two.tile(
                [P, CHUNK * PACK], BF16, name="h_grouped", tag="h_grouped", align_bytes=64
            )
            h_out = h_grouped[c][:].rearrange("q (b i k) -> q b k i", i=RUN, k=PACK)
            cut = (BLOCKS - scalar_blocks(c)) * P // RUN
            if gps(c):
                cut = (BLOCKS - gps(c)) * P // RUN + 2
            nc.vector.tensor_scalar(
                out=h_out[:, :cut],
                in0=h_sum[c][:, :cut],
                scalar1=SQRT_HALF,
                scalar2=None,
                op0=ALU.mult,
            )
            if scalar_blocks(c):
                nc.scalar.activation(
                    out=h_out[:, cut:], in_=h_sum[c][:, cut:], func=ACT.Copy, scale=SQRT_HALF
                )

        def quantise_h(c, part=0, parts=1):
            if part == 0:
                h_codes[c] = two.tile([P, CHUNK], U32, name="h_codes", tag="h_codes", align_bytes=64)
                h_scales[c] = two.tile([P, CHUNK], U8, name="h_scales", tag="h_scales", align_bytes=64)
            words = slice(part * CHUNK // parts, (part + 1) * CHUNK // parts)
            values = slice(part * CHUNK // parts * PACK, (part + 1) * CHUNK // parts * PACK)
            nc.vector.quantize_mx(
                out=h_codes[c][:, words].bitcast(FP8X4),
                scales=h_scales[c][:, words],
                in_=h_grouped[c][:, values],
            )

        def second_product(c, j, copy_out):
            block = slice(j * P, (j + 1) * P)
            n = c // CHUNKS_PER_ITEM
            cols = slice(n * TS, (n + 1) * TS)
            bank = psum.tile([P, TS], F32, name="scores", tag="bank")
            nc.tensor.matmul_mx(
                out=bank[:],
                lhsT=h_codes[c][:, block].bitcast(FP8X4),
                lhsT_scale=h_scales[c][:, block],
                rhs=key_codes[:, cols].bitcast(FP8X4),
                rhs_scale=key_scales[:, cols],
                start=True,
                stop=True,
            )
            if j == 0:
                out_sb[c] = three.tile([P, BLOCKS * TS], F32, name="out_sb", tag="out_sb")
            copy_out(out=out_sb[c][:, j * TS : (j + 1) * TS], in_=bank[:])

        h_banks = {}

        def warm(count):
            bank = psum_h.tile([P, CHUNK], F32, name="warm", tag="bank_h")
            for i in range(count):
                nc.tensor.matmul(
                    out=bank[:], lhsT=zeros[:, 0:P], rhs=zeros[:], start=True, stop=True
                )

        def transposes(c):
            if live(c):
                for half in range(2):
                    copy_te(c, half, transpose_te(c, half))

        def transposes_x(c):
            if live(c):
                for pair in range(2):
                    regroup_x(c, pair, transpose_x(c, pair))

        def products(c, codes):
            if live(c):
                for k in codes:
                    h_banks[c, k] = first_product(c, k)

        def scores(c):
            last = c == CHUNKS - 1
            for j in range(BLOCKS):
                second_product(c, j, nc.vector.tensor_copy if last and j % 2 else nc.scalar.copy)
                if c >= CHUNKS - 2:
                    store_blocks(c, j, 1)
                elif j % 2 == 1:
                    store_blocks(c, j - 1, 2)

        def last_h(c):
            half = BLOCKS // 2
            h_grouped[c] = two.tile(
                [P, CHUNK * PACK], BF16, name="h_grouped", tag="h_grouped", align_bytes=64
            )

            def scale_half(i):
                runs = slice(i * half * P // RUN, (i + 1) * half * P // RUN)
                h_out = h_grouped[c][:].rearrange("q (b i k) -> q b k i", i=RUN, k=PACK)
                nc.vector.tensor_scalar(
                    out=h_out[:, runs],
                    in0=h_sum[c][:, runs],
                    scalar1=SQRT_HALF,
                    scalar2=None,
                    op0=ALU.mult,
                )

            for k in range(PACK):
                sum_h(c, k, h_banks[c, k], 0, half)
            for k in range(2):
                sum_h(c, k, h_banks[c, k], half, BLOCKS)
            scale_half(0)
            for k in range(2, PACK):
                sum_h(c, k, h_banks[c, k], half, BLOCKS)
            quantise_h(c, 0, 2)
            scale_half(1)
            quantise_h(c, 1, 2)

        def pipeline_step(s):
            c_t, c_xq, c_p, c_h = s + T_AHEAD, s + XQ_AHEAD, s + P_AHEAD, s + H_AHEAD
            early = s == CHUNKS - 2

            if early:
                quantise_h(s)
                scores(s)
            if early:
                last_h(c_h)
            elif live(c_h):
                for k in range(PACK):
                    sum_h(c_h, k, h_banks[c_h, k])
            if c_h == 0:
                quantise_x(1)
            n, part = divmod(s, CHUNKS_PER_ITEM)
            if live(s) and (gps(s) or n + 1 < BATCH):
                if gps(s):
                    scale_g(s)
                if n + 1 < BATCH and True:
                    regroup_keys(n + 1, part)

            if s < -1:
                products(c_p, range(PACK))
                transposes_x(c_t)
            else:
                transposes_x(c_t)
                products(c_p, range(2 if s >= 0 else PACK))
            transposes(c_t)
            if s >= 0:
                products(c_p, range(2, PACK))
            if live(s + LOAD_AHEAD):
                load_chunk(s + LOAD_AHEAD)
            c_keys = s + KEYS_AHEAD
            if live(c_keys) and c_keys % CHUNKS_PER_ITEM == 0 and c_keys > CHUNKS_PER_ITEM:
                load_keys(c_keys // CHUNKS_PER_ITEM)

            if live(s):
                if not early and s < CHUNKS - 1:
                    quantise_h(s)
                if s % CHUNKS_PER_ITEM == 0 and s > 0:
                    quantise_keys(s // CHUNKS_PER_ITEM)
            if c_xq > 1 and live(c_xq):
                quantise_x(c_xq)
            if live(c_h) and not early:
                scale_h(c_h)
            if live(s) and not early:
                scores(s)

        v_sb = keep.tile([P, PACK * C], BF16)
        for half in range(2):
            nc.sync.dma_start(
                out=v_sb[:, half * 2 * C : (half + 1) * 2 * C],
                in_=in_proj_v.rearrange("(half m par) c -> half m (par c)", half=2, par=2)[half],
            )
        g_sb = keep.tile([P, PACK], BF16)
        b_sb = keep.tile([P, PACK], BF16)
        with nc.allow_non_contiguous_dma(reason="gain and bias: two pairs of elements a partition"):
            nc.scalar.dma_start(
                out=g_sb[:].rearrange("m (half par) -> m half par", half=2),
                in_=in_proj_g.rearrange("(half m par) -> m half par", half=2, par=2),
            )
            nc.scalar.dma_start(
                out=b_sb[:].rearrange("m (half par) -> m half par", half=2),
                in_=in_proj_b.rearrange("(half m par) -> m half par", half=2, par=2),
            )
        load_chunk(0)
        load_keys(0)
        for c in range(1, IN_BUFS):
            load_chunk(c)
            if c == 3:
                load_keys(1)

        ident_f32 = keep.tile([P, P], F32)
        make_identity(nc, ident_f32[:])

        bias = keep.tile([P, PACK], F32)
        one = keep.tile([P, 1], F32)
        nc.vector.memset(one[:], 1.0)
        zeros = keep.tile([P, CHUNK], BF16)
        nc.vector.memset(zeros[:], 0.0)
        warm(8)
        nc.scalar.sqrt(out=one[:], in_=one[:])
        squares = keep.tile([P, PACK * C], BF16)
        pair_cols = [slice(2 * a, 2 * a + 2) for a in range(2)]
        sum_squares = [keep.tile([P, 2], F32, name="sum_squares%d" % a) for a in range(2)]
        norm = [keep.tile([P, 2], F32, name="norm%d" % a) for a in range(2)]
        inv_norm = [keep.tile([P, 2], F32, name="inv_norm%d" % a) for a in range(2)]
        gain = [keep.tile([P, 2], F32, name="gain%d" % a) for a in range(2)]
        for k in range(PACK):
            group = slice(k * C, (k + 1) * C)
            total = sum_squares[k // 2][:, k % 2 : k % 2 + 1]
            if k < 2:
                nc.scalar.activation(
                    out=squares[:, group], in_=v_sb[:, group], func=ACT.Square, accum_out=total
                )
            else:
                nc.vector.scalar_tensor_tensor(
                    out=squares[:, group],
                    in0=v_sb[:, group],
                    scalar=1.0,
                    in1=v_sb[:, group],
                    op0=ALU.mult,
                    op1=ALU.mult,
                    accum_out=total,
                )
        nc.vector.tensor_copy(out=bias[:], in_=b_sb[:])
        for a in range(2):
            nc.scalar.sqrt(out=norm[a][:], in_=sum_squares[a][:])

        pipeline_step(-T_AHEAD)
        warm(2)

        for a in range(2):
            nc.vector.reciprocal(out=inv_norm[a][:], in_=norm[a][:])
        for a in range(2):
            nc.vector.tensor_tensor(
                out=gain[a][:], in0=inv_norm[a][:], in1=g_sb[:, pair_cols[a]], op=ALU.mult
            )

        w_rows = keep.tile([P, PACK * C], BF16)
        for k in range(PACK):
            nc.vector.tensor_scalar_mul(
                out=w_rows[:, k * C : (k + 1) * C],
                in0=v_sb[:, k * C : (k + 1) * C],
                scalar1=gain[k // 2][:, k % 2 : k % 2 + 1],
            )
        w_words = w_rows[:].bitcast(F32)
        quantise_x(0)
        regroup_keys(0, None)
        w_grouped = keep.tile([P, PACK * P * PACK], BF16, align_bytes=64)
        w_codes = keep.tile([P, PACK * P], U32, align_bytes=64)
        w_scales = keep.tile([P, PACK * P], U8, align_bytes=64)
        for a in range(2):
            pool, tag = (psum, "bank") if a == 0 else (psum_h, "bank_h")
            bank = pool.tile([P, PACK * P], F32, name="wT", tag=tag)
            for i in range(PACK):
                word0 = (a * PACK + i) * P
                nc.tensor.transpose(
                    bank[:, i * P : (i + 1) * P], w_words[:, word0 : word0 + P], ident_f32[:]
                )
            copy_out = nc.scalar.copy if a == 0 else nc.vector.tensor_copy
            copy_out(
                out=w_grouped[:]
                .bitcast(F32)[:, a * C : (a + 1) * C]
                .rearrange("q (g m half) -> q g m half", g=2, half=2),
                in_=bank[:].rearrange("q (g half m) -> q g m half", g=2, half=2),
            )
        for a in range(2):
            words = slice(a * 2 * P, (a + 1) * 2 * P)
            nc.vector.quantize_mx(
                out=w_codes[:, words].bitcast(FP8X4),
                scales=w_scales[:, words],
                in_=w_grouped[:, a * 2 * C : (a + 1) * 2 * C],
            )
        quantise_keys(0)

        warm(2)
        for s in range(1 - T_AHEAD, CHUNKS):
            pipeline_step(s)
